import numpy as np
import ml_dtypes


def mxq(x, axis, fmt="e4m3"):
    dtype, down = {"e4m3": (ml_dtypes.float8_e4m3fn, 7), "e5m2": (ml_dtypes.float8_e5m2, 14)}[fmt]
    v = np.moveaxis(np.asarray(x, np.float32).astype(ml_dtypes.bfloat16).astype(np.float64), axis, -1)
    blocks = v.reshape(v.shape[:-1] + (-1, 32))
    amax = np.abs(blocks).max(-1, keepdims=True)
    byte = np.maximum(np.where(amax > 0, np.frexp(amax)[1] - 1 + 127, 0) - down, 1)
    scale = np.exp2(byte - 127.0)
    codes = (blocks / scale).astype(np.float32).astype(dtype).astype(np.float64)
    return np.moveaxis((codes * scale).reshape(v.shape), -1, axis)


WIDE = False


def mx_kscale(k):
    if not WIDE:
        return np.ones(k)
    levels = np.array([10, -10, 5, -5, 0])
    a = np.random.permutation(np.resize(levels, k // 512 * 4)).reshape(k // 512, 4)
    idx = np.arange(k)
    return np.exp2(a[idx // 512, idx % 128 // 32])


BF16 = ml_dtypes.bfloat16


def bf(x):
    return np.asarray(x, np.float32).astype(BF16)


def f64(x):
    return np.asarray(x).astype(np.float64)


B, S, D, H, F = 8, 1024, 512, 16, 512
EPS = 1e-6


def layernorm(v, gamma, beta):
    mu = v.mean(-1, keepdims=True)
    var = np.square(v - mu).mean(-1, keepdims=True)
    return gamma * (v - mu) * (1.0 / np.sqrt(var + EPS)) + beta


def setup_inputs():
    t = mx_kscale(F)
    n = np.random.standard_normal
    return {"h_attn": bf(n((B, S, D))),
            "w1": bf(n((D, F)) / np.sqrt(D) * t),
            "b1": bf(0.2 * n(F) * t),
            "w2": bf(n((F, D)) / np.sqrt(F) / t[:, None]),
            "b2": bf(0.3 + 0.2 * n(D)),
            "g2": bf(1.0 + 0.1 * n(D)),
            "be2": bf(0.2 * n(D))}


def reference(h_attn, w1, b1, w2, b2, g2, be2):
    y = f64(h_attn)
    h = np.maximum((mxq(y, 2, "e4m3") @ mxq(f64(w1), 0, "e4m3")) + f64(b1), 0.0)
    ffn = (mxq(h, 2, "e4m3") @ mxq(f64(w2), 0, "e4m3")) + f64(b2)
    return layernorm(y + ffn, f64(g2), f64(be2))

@@ -1,0 +1,225 @@
+from contextlib import ExitStack
+
+import concourse.mybir as mybir
+from concourse.masks import make_identity
+
+F32 = mybir.dt.float32
+BF16 = mybir.dt.bfloat16
+U32 = mybir.dt.uint32
+U8 = mybir.dt.uint8
+FP8X4 = mybir.dt.float8_e4m3fn_x4
+ACT = mybir.ActivationFunctionType
+ALU = mybir.AluOpType
+
+P = 128
+PACK = 4
+TOKENS = 8 * 1024
+D = 512
+F = 512
+J = 4
+CHUNK = J * P
+N_CHUNKS = TOKENS // CHUNK
+EPS = 1e-6
+
+FLOPS = 2 * TOKENS * D * F * 2
+
+
+def tile_decoderlayer_pb_t_kernel(tc, h_attn, w1, b1, w2, b2, g2, be2, out):
+    nc = tc.nc
+    x_rows = h_attn.flatten_outer_dims().rearrange("(c p j) d -> c p j d", p=P, j=J)
+    out_rows = out.flatten_outer_dims().rearrange("(c p j) d -> c p j d", p=P, j=J)
+
+    with ExitStack() as stack:
+        const = stack.enter_context(tc.tile_pool(name="const", bufs=1))
+        setup = stack.enter_context(tc.tile_pool(name="setup", bufs=1))
+        work = stack.enter_context(tc.tile_pool(name="work", bufs=2))
+        wide = stack.enter_context(tc.tile_pool(name="wide", bufs=3))
+        small = stack.enter_context(tc.tile_pool(name="small", bufs=4))
+        const_psum = stack.enter_context(tc.psum_pool(name="const_psum", bufs=1))
+        xt_psum = stack.enter_context(tc.psum_pool(name="xt_psum", bufs=2))
+        h_psum = stack.enter_context(tc.psum_pool(name="h_psum", bufs=2))
+        y_psum = stack.enter_context(tc.psum_pool(name="y_psum", bufs=2))
+
+        raw_w1 = setup.tile([P, PACK, F], BF16)
+        for u in range(2):
+            nc.sync.dma_start(
+                out=raw_w1[:, 2 * u : 2 * u + 2, :],
+                in_=w1[256 * u : 256 * u + 256, :].rearrange("(q e) f -> q e f", e=2),
+            )
+        x_all = const.tile([P, N_CHUNKS, J, D], BF16)
+        nc.sync.dma_start(out=x_all[:, 0], in_=x_rows[0])
+        vec_rows = setup.tile([P, 3, D], BF16)
+        nc.vector.memset(vec_rows[:], 0.0)
+        for i, vec in enumerate((b2, g2, be2)):
+            nc.sync.dma_start(out=vec_rows[0:1, i, :], in_=vec.unsqueeze(0))
+        b1_bf = setup.tile([P, PACK], BF16)
+        with nc.allow_non_contiguous_dma(reason="four bias values to a partition"):
+            nc.sync.dma_start(out=b1_bf[:], in_=b1.rearrange("(p m) -> p m", m=PACK))
+        raw_w2 = setup.tile([P, PACK, D], BF16)
+        nc.sync.dma_start(out=raw_w2[:], in_=w2.rearrange("(p t) d -> p t d", t=PACK))
+        for c in range(1, N_CHUNKS):
+            nc.sync.dma_start(out=x_all[:, c], in_=x_rows[c])
+
+        eps_tile = const.tile([P, 1], F32)
+        nc.vector.memset(eps_tile[:], EPS)
+        warm = const.tile([P, 1], F32)
+        nc.scalar.activation(out=warm[:], in_=eps_tile[:], func=ACT.Sqrt)
+        ident = const.tile([P, P], F32)
+        make_identity(nc, ident[:])
+        ones = const.tile([P, P], BF16)
+        nc.vector.memset(ones[:], 1.0)
+
+        grouped_w1 = setup.tile([P, F, PACK], BF16, align_bytes=64)
+        w1_by_m = raw_w1[:].rearrange("p t (i m) -> p m i t", m=PACK)
+        for m in range(PACK):
+            nc.vector.tensor_copy(out=grouped_w1[:, m * P : (m + 1) * P, :], in_=w1_by_m[:, m])
+        w1_codes = const.tile([P, F], U32, align_bytes=64)
+        w1_scales = const.tile([P, F], U8, align_bytes=64)
+        nc.vector.quantize_mx(
+            out=w1_codes[:].bitcast(FP8X4),
+            scales=w1_scales[:],
+            in_=grouped_w1[:].rearrange("p c t -> p (c t)"),
+        )
+        b1_cols = const.tile([P, PACK], F32)
+        nc.vector.tensor_copy(out=b1_cols[:], in_=b1_bf[:])
+
+        grouped_w2 = setup.tile([P, D, PACK], BF16, align_bytes=64)
+        nc.vector.tensor_copy(out=grouped_w2[:], in_=raw_w2[:].rearrange("p t d -> p d t"))
+        w2_codes = const.tile([P, D], U32, align_bytes=64)
+        w2_scales = const.tile([P, D], U8, align_bytes=64)
+        nc.vector.quantize_mx(
+            out=w2_codes[:].bitcast(FP8X4),
+            scales=w2_scales[:],
+            in_=grouped_w2[:].rearrange("p c t -> p (c t)"),
+        )
+
+        b2_ps = y_psum.tile([P, D], F32, tag="y_ps")
+        nc.tensor.matmul(out=b2_ps[:], lhsT=ones[:], rhs=vec_rows[:, 0, :], start=True, stop=True)
+        b2_all = const.tile([P, D], F32)
+        nc.vector.tensor_copy(out=b2_all[:], in_=b2_ps[:])
+        g_ps = const_psum.tile([P, D], F32)
+        nc.tensor.matmul(out=g_ps[:], lhsT=ones[:], rhs=vec_rows[:, 1, :], start=True, stop=True)
+        be_ps = const_psum.tile([P, D], F32)
+        nc.tensor.matmul(out=be_ps[:], lhsT=ones[:], rhs=vec_rows[:, 2, :], start=True, stop=True)
+
+        for c in range(N_CHUNKS):
+            x_chunk = x_all[:, c]
+
+            xb = wide.tile([P, J, D], F32)
+            nc.gpsimd.tensor_tensor(
+                out=xb[:],
+                in0=x_chunk,
+                in1=b2_all[:].unsqueeze(1).to_broadcast([P, J, D]),
+                op=ALU.add,
+            )
+
+            x_words = x_chunk.bitcast(F32)
+            grouped_x = work.tile([P, CHUNK, PACK], BF16, align_bytes=64)
+            gx_words = grouped_x[:].bitcast(F32)
+            for half in range(2):
+                xt = xt_psum.tile([P, 2, 2, P], F32)
+                for jj in range(2):
+                    for u in range(2):
+                        nc.tensor.transpose(
+                            xt[:, jj, u, :],
+                            x_words[:, 2 * half + jj, u * P : (u + 1) * P],
+                            ident[:],
+                        )
+                nc.scalar.copy(
+                    out=gx_words[:, 2 * P * half : 2 * P * (half + 1), :].rearrange(
+                        "p (jj r) u -> p jj r u", jj=2
+                    ),
+                    in_=xt[:].rearrange("p jj u r -> p jj r u"),
+                )
+            x_codes = work.tile([P, CHUNK], U32, align_bytes=64)
+            x_scales = work.tile([P, CHUNK], U8, align_bytes=64)
+            nc.vector.quantize_mx(
+                out=x_codes[:].bitcast(FP8X4),
+                scales=x_scales[:],
+                in_=grouped_x[:].rearrange("p c t -> p (c t)"),
+            )
+
+            h_planes = work.tile([P, PACK, CHUNK], BF16)
+            for m in range(PACK):
+                h_ps = h_psum.tile([P, CHUNK], F32)
+                nc.tensor.matmul_mx(
+                    out=h_ps[:],
+                    lhsT=w1_codes[:, m * P : (m + 1) * P].bitcast(FP8X4),
+                    lhsT_scale=w1_scales[:, m * P : (m + 1) * P],
+                    rhs=x_codes[:].bitcast(FP8X4),
+                    rhs_scale=x_scales[:],
+                    start=True,
+                    stop=True,
+                )
+                nc.scalar.activation(
+                    out=h_planes[:, m, :], in_=h_ps[:], func=ACT.Relu, bias=b1_cols[:, m : m + 1], scale=1.0
+                )
+            grouped_h = work.tile([P, CHUNK, PACK], BF16, align_bytes=64)
+            nc.scalar.copy(out=grouped_h[:], in_=h_planes[:].rearrange("p t c -> p c t"))
+            h_codes = work.tile([P, CHUNK], U32, align_bytes=64)
+            h_scales = work.tile([P, CHUNK], U8, align_bytes=64)
+            nc.vector.quantize_mx(
+                out=h_codes[:].bitcast(FP8X4),
+                scales=h_scales[:],
+                in_=grouped_h[:].rearrange("p c t -> p (c t)"),
+            )
+
+            r = wide.tile([P, J, D], F32)
+            r_sum = small.tile([P, J], F32)
+            for j in range(J):
+                y_ps = y_psum.tile([P, D], F32)
+                nc.tensor.matmul_mx(
+                    out=y_ps[:],
+                    lhsT=h_codes[:, j * P : (j + 1) * P].bitcast(FP8X4),
+                    lhsT_scale=h_scales[:, j * P : (j + 1) * P],
+                    rhs=w2_codes[:].bitcast(FP8X4),
+                    rhs_scale=w2_scales[:],
+                    start=True,
+                    stop=True,
+                )
+                nc.vector.scalar_tensor_tensor(
+                    out=r[:, j, :],
+                    in0=y_ps[:],
+                    scalar=0.0,
+                    in1=xb[:, j, :],
+                    op0=ALU.add,
+                    op1=ALU.add,
+                    accum_out=r_sum[:, j : j + 1],
+                )
+            neg_mean = small.tile([P, J], F32)
+            nc.vector.tensor_scalar_mul(out=neg_mean[:], in0=r_sum[:], scalar1=-1.0 / D)
+            squares = work.tile([P, J, D], BF16)
+            sq_sum = small.tile([P, J], F32)
+            scaled = wide.tile([P, J, D], F32)
+            for j in range(J):
+                nc.scalar.activation(
+                    out=squares[:, j, :],
+                    in_=r[:, j, :],
+                    func=ACT.Square,
+                    bias=neg_mean[:, j : j + 1],
+                    scale=1.0,
+                    accum_out=sq_sum[:, j : j + 1],
+                )
+                nc.vector.scalar_tensor_tensor(
+                    out=scaled[:, j, :],
+                    in0=r[:, j, :],
+                    scalar=neg_mean[:, j : j + 1],
+                    in1=g_ps[:],
+                    op0=ALU.add,
+                    op1=ALU.mult,
+                )
+            std = small.tile([P, J], F32)
+            nc.scalar.activation(out=std[:], in_=sq_sum[:], func=ACT.Sqrt, bias=eps_tile[:], scale=1.0 / D)
+            rstd = small.tile([P, J], F32)
+            nc.vector.reciprocal(out=rstd[:], in_=std[:])
+            result = wide.tile([P, J, D], F32)
+            for j in range(J):
+                nc.vector.scalar_tensor_tensor(
+                    out=result[:, j, :],
+                    in0=scaled[:, j, :],
+                    scalar=rstd[:, j : j + 1],
+                    in1=be_ps[:],
+                    op0=ALU.mult,
+                    op1=ALU.add,
+                )
+            nc.sync.dma_start(out=out_rows[c], in_=result[:])

@@ -31,33 +31,33 @@ def tile_decoderlayer_pb_t_kernel(tc, h_attn, w1, b1, w2, b2, g2, be2, out):
 
     with ExitStack() as stack:
         const = stack.enter_context(tc.tile_pool(name="const", bufs=1))
-        setup = stack.enter_context(tc.tile_pool(name="setup", bufs=1))
         work = stack.enter_context(tc.tile_pool(name="work", bufs=2))
-        wide = stack.enter_context(tc.tile_pool(name="wide", bufs=3))
-        small = stack.enter_context(tc.tile_pool(name="small", bufs=4))
+        per_tile = stack.enter_context(tc.tile_pool(name="per_tile", bufs=J))
+        small = stack.enter_context(tc.tile_pool(name="small", bufs=3))
         const_psum = stack.enter_context(tc.psum_pool(name="const_psum", bufs=1))
         xt_psum = stack.enter_context(tc.psum_pool(name="xt_psum", bufs=2))
         h_psum = stack.enter_context(tc.psum_pool(name="h_psum", bufs=2))
-        y_psum = stack.enter_context(tc.psum_pool(name="y_psum", bufs=2))
+        y_psum = stack.enter_context(tc.psum_pool(name="y_psum", bufs=3))
+        stack.enter_context(tc.manual_schedule())
 
-        raw_w1 = setup.tile([P, PACK, F], BF16)
-        for u in range(2):
-            nc.sync.dma_start(
-                out=raw_w1[:, 2 * u : 2 * u + 2, :],
-                in_=w1[256 * u : 256 * u + 256, :].rearrange("(q e) f -> q e f", e=2),
-            )
         x_all = const.tile([P, N_CHUNKS, J, D], BF16)
         nc.sync.dma_start(out=x_all[:, 0], in_=x_rows[0])
-        vec_rows = setup.tile([P, 3, D], BF16)
+        raw_w1 = const.tile([P, PACK, F], BF16)
+        nc.sync.dma_start(
+            out=raw_w1[:].rearrange("p (u e) f -> p u (e f)", u=2),
+            in_=w1.rearrange("(u q e) f -> q u (e f)", u=2, e=2),
+        )
+        b1_bf = const.tile([P, PACK], BF16)
+        with nc.allow_non_contiguous_dma(reason="four bias values to a partition"):
+            nc.sync.dma_start(out=b1_bf[:], in_=b1.rearrange("(p m) -> p m", m=PACK))
+        nc.sync.dma_start(out=x_all[:, 1], in_=x_rows[1])
+        vec_rows = const.tile([P, 3, D], BF16)
         nc.vector.memset(vec_rows[:], 0.0)
         for i, vec in enumerate((b2, g2, be2)):
             nc.sync.dma_start(out=vec_rows[0:1, i, :], in_=vec.unsqueeze(0))
-        b1_bf = setup.tile([P, PACK], BF16)
-        with nc.allow_non_contiguous_dma(reason="four bias values to a partition"):
-            nc.sync.dma_start(out=b1_bf[:], in_=b1.rearrange("(p m) -> p m", m=PACK))
-        raw_w2 = setup.tile([P, PACK, D], BF16)
+        raw_w2 = const.tile([P, PACK, D], BF16)
         nc.sync.dma_start(out=raw_w2[:], in_=w2.rearrange("(p t) d -> p t d", t=PACK))
-        for c in range(1, N_CHUNKS):
+        for c in range(2, N_CHUNKS):
             nc.sync.dma_start(out=x_all[:, c], in_=x_rows[c])
 
         eps_tile = const.tile([P, 1], F32)
@@ -69,7 +69,7 @@ def tile_decoderlayer_pb_t_kernel(tc, h_attn, w1, b1, w2, b2, g2, be2, out):
         ones = const.tile([P, P], BF16)
         nc.vector.memset(ones[:], 1.0)
 
-        grouped_w1 = setup.tile([P, F, PACK], BF16, align_bytes=64)
+        grouped_w1 = const.tile([P, F, PACK], BF16, align_bytes=64)
         w1_by_m = raw_w1[:].rearrange("p t (i m) -> p m i t", m=PACK)
         for m in range(PACK):
             nc.vector.tensor_copy(out=grouped_w1[:, m * P : (m + 1) * P, :], in_=w1_by_m[:, m])
@@ -83,62 +83,70 @@ def tile_decoderlayer_pb_t_kernel(tc, h_attn, w1, b1, w2, b2, g2, be2, out):
         b1_cols = const.tile([P, PACK], F32)
         nc.vector.tensor_copy(out=b1_cols[:], in_=b1_bf[:])
 
-        grouped_w2 = setup.tile([P, D, PACK], BF16, align_bytes=64)
-        nc.vector.tensor_copy(out=grouped_w2[:], in_=raw_w2[:].rearrange("p t d -> p d t"))
         w2_codes = const.tile([P, D], U32, align_bytes=64)
         w2_scales = const.tile([P, D], U8, align_bytes=64)
-        nc.vector.quantize_mx(
-            out=w2_codes[:].bitcast(FP8X4),
-            scales=w2_scales[:],
-            in_=grouped_w2[:].rearrange("p c t -> p (c t)"),
-        )
-
-        b2_ps = y_psum.tile([P, D], F32, tag="y_ps")
-        nc.tensor.matmul(out=b2_ps[:], lhsT=ones[:], rhs=vec_rows[:, 0, :], start=True, stop=True)
         b2_all = const.tile([P, D], F32)
-        nc.vector.tensor_copy(out=b2_all[:], in_=b2_ps[:])
-        g_ps = const_psum.tile([P, D], F32)
-        nc.tensor.matmul(out=g_ps[:], lhsT=ones[:], rhs=vec_rows[:, 1, :], start=True, stop=True)
-        be_ps = const_psum.tile([P, D], F32)
-        nc.tensor.matmul(out=be_ps[:], lhsT=ones[:], rhs=vec_rows[:, 2, :], start=True, stop=True)
+        gain_shift = const_psum.tile([P, 2, D], BF16)
 
-        for c in range(N_CHUNKS):
-            x_chunk = x_all[:, c]
-
-            xb = wide.tile([P, J, D], F32)
-            nc.gpsimd.tensor_tensor(
-                out=xb[:],
-                in0=x_chunk,
-                in1=b2_all[:].unsqueeze(1).to_broadcast([P, J, D]),
-                op=ALU.add,
+        def prepare_second_half():
+            grouped_w2 = const.tile([P, D, PACK], BF16, align_bytes=64)
+            nc.vector.tensor_copy(out=grouped_w2[:], in_=raw_w2[:].rearrange("p t d -> p d t"))
+            b2_ps = y_psum.tile([P, D], F32, tag="y_ps")
+            nc.tensor.matmul(out=b2_ps[:], lhsT=ones[:], rhs=vec_rows[:, 0, :], start=True, stop=True)
+            nc.vector.tensor_copy(out=b2_all[:], in_=b2_ps[:])
+            for i in range(2):
+                nc.tensor.matmul(
+                    out=gain_shift[:, i, :], lhsT=ones[:], rhs=vec_rows[:, 1 + i, :], start=True, stop=True
+                )
+            nc.vector.quantize_mx(
+                out=w2_codes[:].bitcast(FP8X4),
+                scales=w2_scales[:],
+                in_=grouped_w2[:].rearrange("p c t -> p (c t)"),
             )
 
-            x_words = x_chunk.bitcast(F32)
+        grouped_x_of = {}
+        x_mx_of = {}
+        h_planes_of = {}
+        grouped_h_of = {}
+        h_mx_of = {}
+        xb_of = {}
+        r_of = {}
+        neg_mean_of = {}
+        scaled_of = {}
+        std_of = {}
+
+        def transpose_x(c):
+            x_words = x_all[:, c].bitcast(F32)
             grouped_x = work.tile([P, CHUNK, PACK], BF16, align_bytes=64)
             gx_words = grouped_x[:].bitcast(F32)
+            banks = []
             for half in range(2):
                 xt = xt_psum.tile([P, 2, 2, P], F32)
                 for jj in range(2):
                     for u in range(2):
                         nc.tensor.transpose(
-                            xt[:, jj, u, :],
-                            x_words[:, 2 * half + jj, u * P : (u + 1) * P],
-                            ident[:],
+                            xt[:, jj, u, :], x_words[:, 2 * half + jj, u * P : (u + 1) * P], ident[:]
                         )
+                banks.append(xt)
+            for half in range(2):
                 nc.scalar.copy(
                     out=gx_words[:, 2 * P * half : 2 * P * (half + 1), :].rearrange(
                         "p (jj r) u -> p jj r u", jj=2
                     ),
-                    in_=xt[:].rearrange("p jj u r -> p jj r u"),
+                    in_=banks[half][:].rearrange("p jj u r -> p jj r u"),
                 )
-            x_codes = work.tile([P, CHUNK], U32, align_bytes=64)
-            x_scales = work.tile([P, CHUNK], U8, align_bytes=64)
-            nc.vector.quantize_mx(
-                out=x_codes[:].bitcast(FP8X4),
-                scales=x_scales[:],
-                in_=grouped_x[:].rearrange("p c t -> p (c t)"),
-            )
+            grouped_x_of[c] = grouped_x
 
+        def quantise(grouped):
+            codes = work.tile([P, CHUNK], U32, align_bytes=64, tag="codes", bufs=4)
+            scales = work.tile([P, CHUNK], U8, align_bytes=64, tag="scales", bufs=4)
+            nc.vector.quantize_mx(
+                out=codes[:].bitcast(FP8X4), scales=scales[:], in_=grouped[:].rearrange("p c t -> p (c t)")
+            )
+            return codes, scales
+
+        def first_matmul(c):
+            x_codes, x_scales = x_mx_of[c]
             h_planes = work.tile([P, PACK, CHUNK], BF16)
             for m in range(PACK):
                 h_ps = h_psum.tile([P, CHUNK], F32)
@@ -154,72 +162,110 @@ def tile_decoderlayer_pb_t_kernel(tc, h_attn, w1, b1, w2, b2, g2, be2, out):
                 nc.scalar.activation(
                     out=h_planes[:, m, :], in_=h_ps[:], func=ACT.Relu, bias=b1_cols[:, m : m + 1], scale=1.0
                 )
+            h_planes_of[c] = h_planes
+
+        def regroup_h(c):
             grouped_h = work.tile([P, CHUNK, PACK], BF16, align_bytes=64)
-            nc.scalar.copy(out=grouped_h[:], in_=h_planes[:].rearrange("p t c -> p c t"))
-            h_codes = work.tile([P, CHUNK], U32, align_bytes=64)
-            h_scales = work.tile([P, CHUNK], U8, align_bytes=64)
-            nc.vector.quantize_mx(
-                out=h_codes[:].bitcast(FP8X4),
-                scales=h_scales[:],
-                in_=grouped_h[:].rearrange("p c t -> p (c t)"),
+            nc.scalar.copy(
+                out=grouped_h[:].rearrange("p (c i) t -> p c t i", i=4),
+                in_=h_planes_of[c][:].rearrange("p t (c i) -> p c t i", i=4),
+            )
+            grouped_h_of[c] = grouped_h
+
+        def add_bias_to_x(c, j):
+            xb = per_tile.tile([P, D], F32)
+            nc.gpsimd.tensor_tensor(out=xb[:], in0=x_all[:, c, j, :], in1=b2_all[:], op=ALU.add)
+            xb_of[(c, j)] = xb
+
+        def second_matmul(c, j, r, r_sum):
+            h_codes, h_scales = h_mx_of[c]
+            y_ps = y_psum.tile([P, D], F32)
+            nc.tensor.matmul_mx(
+                out=y_ps[:],
+                lhsT=h_codes[:, j * P : (j + 1) * P].bitcast(FP8X4),
+                lhsT_scale=h_scales[:, j * P : (j + 1) * P],
+                rhs=w2_codes[:].bitcast(FP8X4),
+                rhs_scale=w2_scales[:],
+                start=True,
+                stop=True,
+            )
+            nc.vector.scalar_tensor_tensor(
+                out=r[:, j, :],
+                in0=y_ps[:],
+                scalar=0.0,
+                in1=xb_of[(c, j)][:],
+                op0=ALU.add,
+                op1=ALU.add,
+                accum_out=r_sum[:, j : j + 1],
             )
 
-            r = wide.tile([P, J, D], F32)
-            r_sum = small.tile([P, J], F32)
+        def step(k):
+            if 0 <= k < N_CHUNKS:
+                r = work.tile([P, J, D], F32)
+                r_sum = small.tile([P, J], F32)
+                r_of[k] = r
             for j in range(J):
-                y_ps = y_psum.tile([P, D], F32)
-                nc.tensor.matmul_mx(
-                    out=y_ps[:],
-                    lhsT=h_codes[:, j * P : (j + 1) * P].bitcast(FP8X4),
-                    lhsT_scale=h_scales[:, j * P : (j + 1) * P],
-                    rhs=w2_codes[:].bitcast(FP8X4),
-                    rhs_scale=w2_scales[:],
-                    start=True,
-                    stop=True,
-                )
-                nc.vector.scalar_tensor_tensor(
-                    out=r[:, j, :],
-                    in0=y_ps[:],
-                    scalar=0.0,
-                    in1=xb[:, j, :],
-                    op0=ALU.add,
-                    op1=ALU.add,
-                    accum_out=r_sum[:, j : j + 1],
-                )
-            neg_mean = small.tile([P, J], F32)
-            nc.vector.tensor_scalar_mul(out=neg_mean[:], in0=r_sum[:], scalar1=-1.0 / D)
-            squares = work.tile([P, J, D], BF16)
-            sq_sum = small.tile([P, J], F32)
-            scaled = wide.tile([P, J, D], F32)
-            for j in range(J):
-                nc.scalar.activation(
-                    out=squares[:, j, :],
-                    in_=r[:, j, :],
-                    func=ACT.Square,
-                    bias=neg_mean[:, j : j + 1],
-                    scale=1.0,
-                    accum_out=sq_sum[:, j : j + 1],
-                )
-                nc.vector.scalar_tensor_tensor(
-                    out=scaled[:, j, :],
-                    in0=r[:, j, :],
-                    scalar=neg_mean[:, j : j + 1],
-                    in1=g_ps[:],
-                    op0=ALU.add,
-                    op1=ALU.mult,
-                )
-            std = small.tile([P, J], F32)
-            nc.scalar.activation(out=std[:], in_=sq_sum[:], func=ACT.Sqrt, bias=eps_tile[:], scale=1.0 / D)
-            rstd = small.tile([P, J], F32)
-            nc.vector.reciprocal(out=rstd[:], in_=std[:])
-            result = wide.tile([P, J, D], F32)
-            for j in range(J):
-                nc.vector.scalar_tensor_tensor(
-                    out=result[:, j, :],
-                    in0=scaled[:, j, :],
-                    scalar=rstd[:, j : j + 1],
-                    in1=be_ps[:],
-                    op0=ALU.mult,
-                    op1=ALU.add,
-                )
-            nc.sync.dma_start(out=out_rows[c], in_=result[:])
+                if 0 <= k < N_CHUNKS:
+                    second_matmul(k, j, r, r_sum)
+                if 0 <= k + 1 < N_CHUNKS:
+                    add_bias_to_x(k + 1, j)
+            if 0 <= k < N_CHUNKS:
+                neg_mean = small.tile([P, J], F32)
+                nc.vector.tensor_scalar_mul(out=neg_mean[:], in0=r_sum[:], scalar1=-1.0 / D)
+                neg_mean_of[k] = neg_mean
+            if 0 <= k + 1 < N_CHUNKS:
+                regroup_h(k + 1)
+            if 0 <= k - 1 < N_CHUNKS:
+                rstd = small.tile([P, J], F32)
+                nc.vector.reciprocal(out=rstd[:], in_=std_of[k - 1][:])
+                for j in range(J):
+                    result = per_tile.tile([P, D], F32)
+                    nc.vector.scalar_tensor_tensor(
+                        out=result[:],
+                        in0=scaled_of[k - 1][:, j, :],
+                        scalar=rstd[:, j : j + 1],
+                        in1=gain_shift[:, 1, :],
+                        op0=ALU.mult,
+                        op1=ALU.add,
+                    )
+                    nc.sync.dma_start(out=out_rows[k - 1][:, j, :], in_=result[:])
+            if 0 <= k + 2 < N_CHUNKS:
+                first_matmul(k + 2)
+            if 0 <= k < N_CHUNKS:
+                scaled = work.tile([P, J, D], F32)
+                for j in range(J):
+                    nc.vector.scalar_tensor_tensor(
+                        out=scaled[:, j, :],
+                        in0=r_of[k][:, j, :],
+                        scalar=neg_mean_of[k][:, j : j + 1],
+                        in1=gain_shift[:, 0, :],
+                        op0=ALU.add,
+                        op1=ALU.mult,
+                    )
+                scaled_of[k] = scaled
+                squares = work.tile([P, J, D], BF16)
+                sq_sum = small.tile([P, J], F32)
+                for j in range(J):
+                    nc.scalar.activation(
+                        out=squares[:, j, :],
+                        in_=r_of[k][:, j, :],
+                        func=ACT.Square,
+                        bias=neg_mean_of[k][:, j : j + 1],
+                        scale=1.0,
+                        accum_out=sq_sum[:, j : j + 1],
+                    )
+                std = small.tile([P, J], F32)
+                nc.scalar.activation(out=std[:], in_=sq_sum[:], func=ACT.Sqrt, bias=eps_tile[:], scale=1.0 / D)
+                std_of[k] = std
+            if 0 <= k + 4 < N_CHUNKS:
+                transpose_x(k + 4)
+            if 0 <= k + 1 < N_CHUNKS:
+                h_mx_of[k + 1] = quantise(grouped_h_of[k + 1])
+            if 0 <= k + 3 < N_CHUNKS:
+                x_mx_of[k + 3] = quantise(grouped_x_of[k + 3])
+
+        for k in range(-4, -2):
+            step(k)
+        prepare_second_half()
+        for k in range(-2, N_CHUNKS + 1):
+            step(k)

@@ -35,8 +35,7 @@ def tile_decoderlayer_pb_t_kernel(tc, h_attn, w1, b1, w2, b2, g2, be2, out):
         per_tile = stack.enter_context(tc.tile_pool(name="per_tile", bufs=J))
         small = stack.enter_context(tc.tile_pool(name="small", bufs=3))
         const_psum = stack.enter_context(tc.psum_pool(name="const_psum", bufs=1))
-        xt_psum = stack.enter_context(tc.psum_pool(name="xt_psum", bufs=2))
-        h_psum = stack.enter_context(tc.psum_pool(name="h_psum", bufs=2))
+        front_psum = stack.enter_context(tc.psum_pool(name="front_psum", bufs=4))
         y_psum = stack.enter_context(tc.psum_pool(name="y_psum", bufs=3))
         stack.enter_context(tc.manual_schedule())
 
@@ -121,7 +120,7 @@ def tile_decoderlayer_pb_t_kernel(tc, h_attn, w1, b1, w2, b2, g2, be2, out):
             gx_words = grouped_x[:].bitcast(F32)
             banks = []
             for half in range(2):
-                xt = xt_psum.tile([P, 2, 2, P], F32)
+                xt = front_psum.tile([P, 2, 2, P], F32, tag="front")
                 for jj in range(2):
                     for u in range(2):
                         nc.tensor.transpose(
@@ -149,7 +148,7 @@ def tile_decoderlayer_pb_t_kernel(tc, h_attn, w1, b1, w2, b2, g2, be2, out):
             x_codes, x_scales = x_mx_of[c]
             h_planes = work.tile([P, PACK, CHUNK], BF16)
             for m in range(PACK):
-                h_ps = h_psum.tile([P, CHUNK], F32)
+                h_ps = front_psum.tile([P, CHUNK], F32, tag="front")
                 nc.tensor.matmul_mx(
                     out=h_ps[:],
                     lhsT=w1_codes[:, m * P : (m + 1) * P].bitcast(FP8X4),
@@ -199,6 +198,16 @@ def tile_decoderlayer_pb_t_kernel(tc, h_attn, w1, b1, w2, b2, g2, be2, out):
                 accum_out=r_sum[:, j : j + 1],
             )
 
+        def gain(c, j):
+            nc.vector.scalar_tensor_tensor(
+                out=scaled_of[c][:, j, :],
+                in0=r_of[c][:, j, :],
+                scalar=neg_mean_of[c][:, j : j + 1],
+                in1=gain_shift[:, 0, :],
+                op0=ALU.add,
+                op1=ALU.mult,
+            )
+
         def step(k):
             if 0 <= k < N_CHUNKS:
                 r = work.tile([P, J, D], F32)
@@ -209,6 +218,9 @@ def tile_decoderlayer_pb_t_kernel(tc, h_attn, w1, b1, w2, b2, g2, be2, out):
                     second_matmul(k, j, r, r_sum)
                 if 0 <= k + 1 < N_CHUNKS:
                     add_bias_to_x(k + 1, j)
+            if 0 <= k - 1 < N_CHUNKS:
+                rstd = small.tile([P, J], F32)
+                nc.vector.reciprocal(out=rstd[:], in_=std_of[k - 1][:])
             if 0 <= k < N_CHUNKS:
                 neg_mean = small.tile([P, J], F32)
                 nc.vector.tensor_scalar_mul(out=neg_mean[:], in0=r_sum[:], scalar1=-1.0 / D)
@@ -216,8 +228,6 @@ def tile_decoderlayer_pb_t_kernel(tc, h_attn, w1, b1, w2, b2, g2, be2, out):
             if 0 <= k + 1 < N_CHUNKS:
                 regroup_h(k + 1)
             if 0 <= k - 1 < N_CHUNKS:
-                rstd = small.tile([P, J], F32)
-                nc.vector.reciprocal(out=rstd[:], in_=std_of[k - 1][:])
                 for j in range(J):
                     result = per_tile.tile([P, D], F32)
                     nc.vector.scalar_tensor_tensor(
@@ -233,16 +243,16 @@ def tile_decoderlayer_pb_t_kernel(tc, h_attn, w1, b1, w2, b2, g2, be2, out):
                 first_matmul(k + 2)
             if 0 <= k < N_CHUNKS:
                 scaled = work.tile([P, J, D], F32)
-                for j in range(J):
-                    nc.vector.scalar_tensor_tensor(
-                        out=scaled[:, j, :],
-                        in0=r_of[k][:, j, :],
-                        scalar=neg_mean_of[k][:, j : j + 1],
-                        in1=gain_shift[:, 0, :],
-                        op0=ALU.add,
-                        op1=ALU.mult,
-                    )
                 scaled_of[k] = scaled
+                gain(k, 0)
+                gain(k, 1)
+            if 0 <= k + 1 < N_CHUNKS:
+                h_mx_of[k + 1] = quantise(grouped_h_of[k + 1])
+            if 0 <= k + 3 < N_CHUNKS:
+                x_mx_of[k + 3] = quantise(grouped_x_of[k + 3])
+            if 0 <= k < N_CHUNKS:
+                gain(k, 2)
+                gain(k, 3)
                 squares = work.tile([P, J, D], BF16)
                 sq_sum = small.tile([P, J], F32)
                 for j in range(J):
@@ -254,15 +264,12 @@ def tile_decoderlayer_pb_t_kernel(tc, h_attn, w1, b1, w2, b2, g2, be2, out):
                         scale=1.0,
                         accum_out=sq_sum[:, j : j + 1],
                     )
+            if 0 <= k + 4 < N_CHUNKS:
+                transpose_x(k + 4)
+            if 0 <= k < N_CHUNKS:
                 std = small.tile([P, J], F32)
                 nc.scalar.activation(out=std[:], in_=sq_sum[:], func=ACT.Sqrt, bias=eps_tile[:], scale=1.0 / D)
                 std_of[k] = std
-            if 0 <= k + 4 < N_CHUNKS:
-                transpose_x(k + 4)
-            if 0 <= k + 1 < N_CHUNKS:
-                h_mx_of[k + 1] = quantise(grouped_h_of[k + 1])
-            if 0 <= k + 3 < N_CHUNKS:
-                x_mx_of[k + 3] = quantise(grouped_x_of[k + 3])
 
         for k in range(-4, -2):
             step(k)

@@ -39,13 +39,13 @@ def tile_decoderlayer_pb_t_kernel(tc, h_attn, w1, b1, w2, b2, g2, be2, out):
         y_psum = stack.enter_context(tc.psum_pool(name="y_psum", bufs=3))
         stack.enter_context(tc.manual_schedule())
 
-        x_all = const.tile([P, N_CHUNKS, J, D], BF16)
-        nc.sync.dma_start(out=x_all[:, 0], in_=x_rows[0])
         raw_w1 = const.tile([P, PACK, F], BF16)
         nc.sync.dma_start(
             out=raw_w1[:].rearrange("p (u e) f -> p u (e f)", u=2),
             in_=w1.rearrange("(u q e) f -> q u (e f)", u=2, e=2),
         )
+        x_all = const.tile([P, N_CHUNKS, J, D], BF16)
+        nc.sync.dma_start(out=x_all[:, 0], in_=x_rows[0])
         b1_bf = const.tile([P, PACK], BF16)
         with nc.allow_non_contiguous_dma(reason="four bias values to a partition"):
             nc.sync.dma_start(out=b1_bf[:], in_=b1.rearrange("(p m) -> p m", m=PACK))
@@ -62,7 +62,7 @@ def tile_decoderlayer_pb_t_kernel(tc, h_attn, w1, b1, w2, b2, g2, be2, out):
         eps_tile = const.tile([P, 1], F32)
         nc.vector.memset(eps_tile[:], EPS)
         warm = const.tile([P, 1], F32)
-        nc.scalar.activation(out=warm[:], in_=eps_tile[:], func=ACT.Sqrt)
+        nc.scalar.activation(out=warm[:], in_=eps_tile[:], func=ACT.Abs_reciprocal_sqrt)
         ident = const.tile([P, P], F32)
         make_identity(nc, ident[:])
         ones = const.tile([P, P], BF16)
@@ -112,9 +112,9 @@ def tile_decoderlayer_pb_t_kernel(tc, h_attn, w1, b1, w2, b2, g2, be2, out):
         r_of = {}
         neg_mean_of = {}
         scaled_of = {}
-        std_of = {}
+        rstd_of = {}
 
-        def transpose_x(c):
+        def transpose_x(c, copy):
             x_words = x_all[:, c].bitcast(F32)
             grouped_x = work.tile([P, CHUNK, PACK], BF16, align_bytes=64)
             gx_words = grouped_x[:].bitcast(F32)
@@ -128,7 +128,7 @@ def tile_decoderlayer_pb_t_kernel(tc, h_attn, w1, b1, w2, b2, g2, be2, out):
                         )
                 banks.append(xt)
             for half in range(2):
-                nc.scalar.copy(
+                copy(
                     out=gx_words[:, 2 * P * half : 2 * P * (half + 1), :].rearrange(
                         "p (jj r) u -> p jj r u", jj=2
                     ),
@@ -163,9 +163,9 @@ def tile_decoderlayer_pb_t_kernel(tc, h_attn, w1, b1, w2, b2, g2, be2, out):
                 )
             h_planes_of[c] = h_planes
 
-        def regroup_h(c):
+        def regroup_h(c, copy):
             grouped_h = work.tile([P, CHUNK, PACK], BF16, align_bytes=64)
-            nc.scalar.copy(
+            copy(
                 out=grouped_h[:].rearrange("p (c i) t -> p c t i", i=4),
                 in_=h_planes_of[c][:].rearrange("p t (c i) -> p c t i", i=4),
             )
@@ -209,6 +209,7 @@ def tile_decoderlayer_pb_t_kernel(tc, h_attn, w1, b1, w2, b2, g2, be2, out):
             )
 
         def step(k):
+            copy = nc.vector.tensor_copy if k < 0 else nc.scalar.copy
             if 0 <= k < N_CHUNKS:
                 r = work.tile([P, J, D], F32)
                 r_sum = small.tile([P, J], F32)
@@ -218,22 +219,19 @@ def tile_decoderlayer_pb_t_kernel(tc, h_attn, w1, b1, w2, b2, g2, be2, out):
                     second_matmul(k, j, r, r_sum)
                 if 0 <= k + 1 < N_CHUNKS:
                     add_bias_to_x(k + 1, j)
-            if 0 <= k - 1 < N_CHUNKS:
-                rstd = small.tile([P, J], F32)
-                nc.vector.reciprocal(out=rstd[:], in_=std_of[k - 1][:])
             if 0 <= k < N_CHUNKS:
                 neg_mean = small.tile([P, J], F32)
                 nc.vector.tensor_scalar_mul(out=neg_mean[:], in0=r_sum[:], scalar1=-1.0 / D)
                 neg_mean_of[k] = neg_mean
             if 0 <= k + 1 < N_CHUNKS:
-                regroup_h(k + 1)
+                regroup_h(k + 1, copy)
             if 0 <= k - 1 < N_CHUNKS:
                 for j in range(J):
                     result = per_tile.tile([P, D], F32)
                     nc.vector.scalar_tensor_tensor(
                         out=result[:],
                         in0=scaled_of[k - 1][:, j, :],
-                        scalar=rstd[:, j : j + 1],
+                        scalar=rstd_of[k - 1][:, j : j + 1],
                         in1=gain_shift[:, 1, :],
                         op0=ALU.mult,
                         op1=ALU.add,
@@ -265,11 +263,13 @@ def tile_decoderlayer_pb_t_kernel(tc, h_attn, w1, b1, w2, b2, g2, be2, out):
                         accum_out=sq_sum[:, j : j + 1],
                     )
             if 0 <= k + 4 < N_CHUNKS:
-                transpose_x(k + 4)
+                transpose_x(k + 4, copy)
             if 0 <= k < N_CHUNKS:
-                std = small.tile([P, J], F32)
-                nc.scalar.activation(out=std[:], in_=sq_sum[:], func=ACT.Sqrt, bias=eps_tile[:], scale=1.0 / D)
-                std_of[k] = std
+                rstd = small.tile([P, J], F32)
+                nc.scalar.activation(
+                    out=rstd[:], in_=sq_sum[:], func=ACT.Abs_reciprocal_sqrt, bias=eps_tile[:], scale=1.0 / D
+                )
+                rstd_of[k] = rstd
 
         for k in range(-4, -2):
             step(k)

@@ -16,9 +16,10 @@ PACK = 4
 TOKENS = 8 * 1024
 D = 512
 F = 512
-J = 4
-CHUNK = J * P
-N_CHUNKS = TOKENS // CHUNK
+TILES = TOKENS // P
+CHUNK_TILES = [2] + [4] * 15 + [2]
+N_CHUNKS = len(CHUNK_TILES)
+FIRST_TILE = [sum(CHUNK_TILES[:c]) for c in range(N_CHUNKS)]
 EPS = 1e-6
 
 FLOPS = 2 * TOKENS * D * F * 2
@@ -26,30 +27,39 @@ FLOPS = 2 * TOKENS * D * F * 2
 
 def tile_decoderlayer_pb_t_kernel(tc, h_attn, w1, b1, w2, b2, g2, be2, out):
     nc = tc.nc
-    x_rows = h_attn.flatten_outer_dims().rearrange("(c p j) d -> c p j d", p=P, j=J)
-    out_rows = out.flatten_outer_dims().rearrange("(c p j) d -> c p j d", p=P, j=J)
+    x_flat = h_attn.flatten_outer_dims()
+    out_flat = out.flatten_outer_dims()
+
+    def rows_of(flat, c):
+        jn = CHUNK_TILES[c]
+        first = FIRST_TILE[c] * P
+        return flat[first : first + jn * P, :].rearrange("(p j) d -> p j d", j=jn)
 
     with ExitStack() as stack:
         const = stack.enter_context(tc.tile_pool(name="const", bufs=1))
         work = stack.enter_context(tc.tile_pool(name="work", bufs=2))
-        per_tile = stack.enter_context(tc.tile_pool(name="per_tile", bufs=J))
+        per_tile = stack.enter_context(tc.tile_pool(name="per_tile", bufs=4))
         small = stack.enter_context(tc.tile_pool(name="small", bufs=3))
         const_psum = stack.enter_context(tc.psum_pool(name="const_psum", bufs=1))
         front_psum = stack.enter_context(tc.psum_pool(name="front_psum", bufs=4))
         y_psum = stack.enter_context(tc.psum_pool(name="y_psum", bufs=3))
         stack.enter_context(tc.manual_schedule())
 
+        x_all = const.tile([P, TILES, D], BF16)
+
+        def x_of(c):
+            return x_all[:, FIRST_TILE[c] : FIRST_TILE[c] + CHUNK_TILES[c]]
+
         raw_w1 = const.tile([P, PACK, F], BF16)
         nc.sync.dma_start(
             out=raw_w1[:].rearrange("p (u e) f -> p u (e f)", u=2),
             in_=w1.rearrange("(u q e) f -> q u (e f)", u=2, e=2),
         )
-        x_all = const.tile([P, N_CHUNKS, J, D], BF16)
-        nc.sync.dma_start(out=x_all[:, 0], in_=x_rows[0])
+        nc.sync.dma_start(out=x_of(0), in_=rows_of(x_flat, 0))
         b1_bf = const.tile([P, PACK], BF16)
         with nc.allow_non_contiguous_dma(reason="four bias values to a partition"):
             nc.sync.dma_start(out=b1_bf[:], in_=b1.rearrange("(p m) -> p m", m=PACK))
-        nc.sync.dma_start(out=x_all[:, 1], in_=x_rows[1])
+        nc.sync.dma_start(out=x_of(1), in_=rows_of(x_flat, 1))
         vec_rows = const.tile([P, 3, D], BF16)
         nc.vector.memset(vec_rows[:], 0.0)
         for i, vec in enumerate((b2, g2, be2)):
@@ -57,7 +67,7 @@ def tile_decoderlayer_pb_t_kernel(tc, h_attn, w1, b1, w2, b2, g2, be2, out):
         raw_w2 = const.tile([P, PACK, D], BF16)
         nc.sync.dma_start(out=raw_w2[:], in_=w2.rearrange("(p t) d -> p t d", t=PACK))
         for c in range(2, N_CHUNKS):
-            nc.sync.dma_start(out=x_all[:, c], in_=x_rows[c])
+            nc.sync.dma_start(out=x_of(c), in_=rows_of(x_flat, c))
 
         eps_tile = const.tile([P, 1], F32)
         nc.vector.memset(eps_tile[:], EPS)
@@ -71,7 +81,8 @@ def tile_decoderlayer_pb_t_kernel(tc, h_attn, w1, b1, w2, b2, g2, be2, out):
         grouped_w1 = const.tile([P, F, PACK], BF16, align_bytes=64)
         w1_by_m = raw_w1[:].rearrange("p t (i m) -> p m i t", m=PACK)
         for m in range(PACK):
-            nc.vector.tensor_copy(out=grouped_w1[:, m * P : (m + 1) * P, :], in_=w1_by_m[:, m])
+            w1_copy = nc.scalar.copy if m == 3 else nc.vector.tensor_copy
+            w1_copy(out=grouped_w1[:, m * P : (m + 1) * P, :], in_=w1_by_m[:, m])
         w1_codes = const.tile([P, F], U32, align_bytes=64)
         w1_scales = const.tile([P, F], U8, align_bytes=64)
         nc.vector.quantize_mx(
@@ -80,23 +91,34 @@ def tile_decoderlayer_pb_t_kernel(tc, h_attn, w1, b1, w2, b2, g2, be2, out):
             in_=grouped_w1[:].rearrange("p c t -> p (c t)"),
         )
         b1_cols = const.tile([P, PACK], F32)
-        nc.vector.tensor_copy(out=b1_cols[:], in_=b1_bf[:])
+        nc.gpsimd.tensor_copy(out=b1_cols[:], in_=b1_bf[:])
 
+        grouped_w2 = const.tile([P, D, PACK], BF16, align_bytes=64)
         w2_codes = const.tile([P, D], U32, align_bytes=64)
         w2_scales = const.tile([P, D], U8, align_bytes=64)
-        b2_all = const.tile([P, D], F32)
+        b2_all = const.tile([P, D], BF16)
         gain_shift = const_psum.tile([P, 2, D], BF16)
 
-        def prepare_second_half():
-            grouped_w2 = const.tile([P, D, PACK], BF16, align_bytes=64)
-            nc.vector.tensor_copy(out=grouped_w2[:], in_=raw_w2[:].rearrange("p t d -> p d t"))
-            b2_ps = y_psum.tile([P, D], F32, tag="y_ps")
+        def group_w2():
+            nc.gpsimd.tensor_scalar(
+                out=grouped_w2[:],
+                in0=raw_w2[:].rearrange("p t d -> p d t"),
+                scalar1=1.0,
+                scalar2=0.0,
+                op0=ALU.mult,
+                op1=ALU.add,
+            )
+
+        def broadcast_vectors():
+            b2_ps = y_psum.tile([P, D], BF16, tag="y_ps")
             nc.tensor.matmul(out=b2_ps[:], lhsT=ones[:], rhs=vec_rows[:, 0, :], start=True, stop=True)
-            nc.vector.tensor_copy(out=b2_all[:], in_=b2_ps[:])
+            nc.scalar.copy(out=b2_all[:], in_=b2_ps[:])
             for i in range(2):
                 nc.tensor.matmul(
                     out=gain_shift[:, i, :], lhsT=ones[:], rhs=vec_rows[:, 1 + i, :], start=True, stop=True
                 )
+
+        def quantise_w2():
             nc.vector.quantize_mx(
                 out=w2_codes[:].bitcast(FP8X4),
                 scales=w2_scales[:],
@@ -110,45 +132,54 @@ def tile_decoderlayer_pb_t_kernel(tc, h_attn, w1, b1, w2, b2, g2, be2, out):
         h_mx_of = {}
         xb_of = {}
         r_of = {}
+        r_sum_of = {}
         neg_mean_of = {}
         scaled_of = {}
         rstd_of = {}
 
         def transpose_x(c, copy):
-            x_words = x_all[:, c].bitcast(F32)
-            grouped_x = work.tile([P, CHUNK, PACK], BF16, align_bytes=64)
+            x_words = x_of(c).bitcast(F32)
+            width = CHUNK_TILES[c] * P
+            grouped_x = work.tile([P, width, PACK], BF16, align_bytes=64)
             gx_words = grouped_x[:].bitcast(F32)
+            pairs = CHUNK_TILES[c] // 2
             banks = []
-            for half in range(2):
+            for pair in range(pairs):
                 xt = front_psum.tile([P, 2, 2, P], F32, tag="front")
                 for jj in range(2):
                     for u in range(2):
                         nc.tensor.transpose(
-                            xt[:, jj, u, :], x_words[:, 2 * half + jj, u * P : (u + 1) * P], ident[:]
+                            xt[:, jj, u, :], x_words[:, 2 * pair + jj, u * P : (u + 1) * P], ident[:]
                         )
                 banks.append(xt)
-            for half in range(2):
+            for pair in range(pairs):
                 copy(
-                    out=gx_words[:, 2 * P * half : 2 * P * (half + 1), :].rearrange(
-                        "p (jj r) u -> p jj r u", jj=2
-                    ),
-                    in_=banks[half][:].rearrange("p jj u r -> p jj r u"),
+                    out=gx_words[:, 2 * P * pair : 2 * P * (pair + 1), :].rearrange("p (jj r) u -> p jj r u", jj=2),
+                    in_=banks[pair][:].rearrange("p jj u r -> p jj r u"),
                 )
             grouped_x_of[c] = grouped_x
 
-        def quantise(grouped):
-            codes = work.tile([P, CHUNK], U32, align_bytes=64, tag="codes", bufs=4)
-            scales = work.tile([P, CHUNK], U8, align_bytes=64, tag="scales", bufs=4)
+        def quantise(grouped, c):
+            width = CHUNK_TILES[c] * P
+            codes = work.tile([P, width], U32, align_bytes=64, tag="codes", bufs=4)
+            scales = work.tile([P, width], U8, align_bytes=64, tag="scales", bufs=4)
             nc.vector.quantize_mx(
                 out=codes[:].bitcast(FP8X4), scales=scales[:], in_=grouped[:].rearrange("p c t -> p (c t)")
             )
             return codes, scales
 
-        def first_matmul(c):
+        def quantise_x(c):
+            x_mx_of[c] = quantise(grouped_x_of[c], c)
+
+        def quantise_h(c):
+            h_mx_of[c] = quantise(grouped_h_of[c], c)
+
+        def first_matmul(c, vector_planes=()):
             x_codes, x_scales = x_mx_of[c]
-            h_planes = work.tile([P, PACK, CHUNK], BF16)
+            width = CHUNK_TILES[c] * P
+            h_planes = work.tile([P, PACK, width], BF16)
             for m in range(PACK):
-                h_ps = front_psum.tile([P, CHUNK], F32, tag="front")
+                h_ps = front_psum.tile([P, width], F32, tag="front")
                 nc.tensor.matmul_mx(
                     out=h_ps[:],
                     lhsT=w1_codes[:, m * P : (m + 1) * P].bitcast(FP8X4),
@@ -158,13 +189,23 @@ def tile_decoderlayer_pb_t_kernel(tc, h_attn, w1, b1, w2, b2, g2, be2, out):
                     start=True,
                     stop=True,
                 )
-                nc.scalar.activation(
-                    out=h_planes[:, m, :], in_=h_ps[:], func=ACT.Relu, bias=b1_cols[:, m : m + 1], scale=1.0
-                )
+                if m in vector_planes:
+                    nc.vector.tensor_scalar(
+                        out=h_planes[:, m, :],
+                        in0=h_ps[:],
+                        scalar1=b1_cols[:, m : m + 1],
+                        scalar2=0.0,
+                        op0=ALU.add,
+                        op1=ALU.max,
+                    )
+                else:
+                    nc.scalar.activation(
+                        out=h_planes[:, m, :], in_=h_ps[:], func=ACT.Relu, bias=b1_cols[:, m : m + 1], scale=1.0
+                    )
             h_planes_of[c] = h_planes
 
         def regroup_h(c, copy):
-            grouped_h = work.tile([P, CHUNK, PACK], BF16, align_bytes=64)
+            grouped_h = work.tile([P, CHUNK_TILES[c] * P, PACK], BF16, align_bytes=64)
             copy(
                 out=grouped_h[:].rearrange("p (c i) t -> p c t i", i=4),
                 in_=h_planes_of[c][:].rearrange("p t (c i) -> p c t i", i=4),
@@ -173,10 +214,16 @@ def tile_decoderlayer_pb_t_kernel(tc, h_attn, w1, b1, w2, b2, g2, be2, out):
 
         def add_bias_to_x(c, j):
             xb = per_tile.tile([P, D], F32)
-            nc.gpsimd.tensor_tensor(out=xb[:], in0=x_all[:, c, j, :], in1=b2_all[:], op=ALU.add)
+            nc.gpsimd.tensor_tensor(out=xb[:], in0=x_of(c)[:, j, :], in1=b2_all[:], op=ALU.add)
             xb_of[(c, j)] = xb
 
-        def second_matmul(c, j, r, r_sum):
+        def start_residual(c):
+            r = work.tile([P, CHUNK_TILES[c], D], F32)
+            r_sum = small.tile([P, CHUNK_TILES[c]], F32)
+            r_of[c] = r
+            r_sum_of[c] = r_sum
+
+        def second_matmul(c, j):
             h_codes, h_scales = h_mx_of[c]
             y_ps = y_psum.tile([P, D], F32)
             nc.tensor.matmul_mx(
@@ -189,14 +236,19 @@ def tile_decoderlayer_pb_t_kernel(tc, h_attn, w1, b1, w2, b2, g2, be2, out):
                 stop=True,
             )
             nc.vector.scalar_tensor_tensor(
-                out=r[:, j, :],
+                out=r_of[c][:, j, :],
                 in0=y_ps[:],
                 scalar=0.0,
                 in1=xb_of[(c, j)][:],
                 op0=ALU.add,
                 op1=ALU.add,
-                accum_out=r_sum[:, j : j + 1],
+                accum_out=r_sum_of[c][:, j : j + 1],
             )
+
+        def negate_mean(c):
+            neg_mean = small.tile([P, CHUNK_TILES[c]], F32)
+            nc.gpsimd.tensor_scalar_mul(out=neg_mean[:], in0=r_sum_of[c][:], scalar1=-1.0 / D)
+            neg_mean_of[c] = neg_mean
 
         def gain(c, j):
             nc.vector.scalar_tensor_tensor(
@@ -208,71 +260,97 @@ def tile_decoderlayer_pb_t_kernel(tc, h_attn, w1, b1, w2, b2, g2, be2, out):
                 op1=ALU.mult,
             )
 
+        def square(c, j, squares, sq_sum):
+            nc.scalar.activation(
+                out=squares[:, j, :],
+                in_=r_of[c][:, j, :],
+                func=ACT.Square,
+                bias=neg_mean_of[c][:, j : j + 1],
+                scale=1.0,
+                accum_out=sq_sum[:, j : j + 1],
+            )
+
+        def deviation(rstd, sq_sum, j0, j1):
+            nc.scalar.activation(
+                out=rstd[:, j0:j1], in_=sq_sum[:, j0:j1], func=ACT.Abs_reciprocal_sqrt, bias=eps_tile[:], scale=1.0 / D
+            )
+
+        def shift_and_store(c):
+            for j in range(CHUNK_TILES[c]):
+                result = per_tile.tile([P, D], F32)
+                nc.vector.scalar_tensor_tensor(
+                    out=result[:],
+                    in0=scaled_of[c][:, j, :],
+                    scalar=rstd_of[c][:, j : j + 1],
+                    in1=gain_shift[:, 1, :],
+                    op0=ALU.mult,
+                    op1=ALU.add,
+                )
+                nc.sync.dma_start(out=rows_of(out_flat, c)[:, j, :], in_=result[:])
+
         def step(k):
-            copy = nc.vector.tensor_copy if k < 0 else nc.scalar.copy
-            if 0 <= k < N_CHUNKS:
-                r = work.tile([P, J, D], F32)
-                r_sum = small.tile([P, J], F32)
-                r_of[k] = r
-            for j in range(J):
-                if 0 <= k < N_CHUNKS:
-                    second_matmul(k, j, r, r_sum)
-                if 0 <= k + 1 < N_CHUNKS:
+            has_residual = k < N_CHUNKS
+            tiles = CHUNK_TILES[k] if has_residual else 0
+            next_tiles = CHUNK_TILES[k + 1] if k + 1 < N_CHUNKS else 0
+            copy = nc.vector.tensor_copy if k == 0 else nc.scalar.copy
+            if has_residual:
+                start_residual(k)
+            for j in range(max(tiles, min(next_tiles, 2))):
+                if j < tiles:
+                    second_matmul(k, j)
+                if j < min(next_tiles, 2):
                     add_bias_to_x(k + 1, j)
-            if 0 <= k < N_CHUNKS:
-                neg_mean = small.tile([P, J], F32)
-                nc.vector.tensor_scalar_mul(out=neg_mean[:], in0=r_sum[:], scalar1=-1.0 / D)
-                neg_mean_of[k] = neg_mean
-            if 0 <= k + 1 < N_CHUNKS:
+            if has_residual:
+                negate_mean(k)
+            for j in range(2, next_tiles):
+                add_bias_to_x(k + 1, j)
+            if k + 1 < N_CHUNKS:
                 regroup_h(k + 1, copy)
-            if 0 <= k - 1 < N_CHUNKS:
-                for j in range(J):
-                    result = per_tile.tile([P, D], F32)
-                    nc.vector.scalar_tensor_tensor(
-                        out=result[:],
-                        in0=scaled_of[k - 1][:, j, :],
-                        scalar=rstd_of[k - 1][:, j : j + 1],
-                        in1=gain_shift[:, 1, :],
-                        op0=ALU.mult,
-                        op1=ALU.add,
-                    )
-                    nc.sync.dma_start(out=out_rows[k - 1][:, j, :], in_=result[:])
-            if 0 <= k + 2 < N_CHUNKS:
+            if k >= 1:
+                shift_and_store(k - 1)
+            if k + 2 < N_CHUNKS:
                 first_matmul(k + 2)
-            if 0 <= k < N_CHUNKS:
-                scaled = work.tile([P, J, D], F32)
+            if has_residual:
+                scaled = work.tile([P, tiles, D], F32)
                 scaled_of[k] = scaled
                 gain(k, 0)
                 gain(k, 1)
-            if 0 <= k + 1 < N_CHUNKS:
-                h_mx_of[k + 1] = quantise(grouped_h_of[k + 1])
-            if 0 <= k + 3 < N_CHUNKS:
-                x_mx_of[k + 3] = quantise(grouped_x_of[k + 3])
-            if 0 <= k < N_CHUNKS:
-                gain(k, 2)
-                gain(k, 3)
-                squares = work.tile([P, J, D], BF16)
-                sq_sum = small.tile([P, J], F32)
-                for j in range(J):
-                    nc.scalar.activation(
-                        out=squares[:, j, :],
-                        in_=r_of[k][:, j, :],
-                        func=ACT.Square,
-                        bias=neg_mean_of[k][:, j : j + 1],
-                        scale=1.0,
-                        accum_out=sq_sum[:, j : j + 1],
-                    )
-            if 0 <= k + 4 < N_CHUNKS:
+            if k + 1 < N_CHUNKS:
+                quantise_h(k + 1)
+            if k + 3 < N_CHUNKS:
+                quantise_x(k + 3)
+            if has_residual:
+                for j in range(2, tiles):
+                    gain(k, j)
+                squares = work.tile([P, tiles, D], BF16)
+                sq_sum = small.tile([P, tiles], F32)
+                rstd = small.tile([P, tiles], F32)
+                for j in range(tiles):
+                    square(k, j, squares, sq_sum)
+                    if k == N_CHUNKS - 1:
+                        deviation(rstd, sq_sum, j, j + 1)
+            if k + 4 < N_CHUNKS:
                 transpose_x(k + 4, copy)
-            if 0 <= k < N_CHUNKS:
-                rstd = small.tile([P, J], F32)
-                nc.scalar.activation(
-                    out=rstd[:], in_=sq_sum[:], func=ACT.Abs_reciprocal_sqrt, bias=eps_tile[:], scale=1.0 / D
-                )
+            if has_residual:
+                if k < N_CHUNKS - 1:
+                    deviation(rstd, sq_sum, 0, tiles)
                 rstd_of[k] = rstd
 
-        for k in range(-4, -2):
-            step(k)
-        prepare_second_half()
-        for k in range(-2, N_CHUNKS + 1):
+        transpose_x(0, nc.scalar.copy)
+        quantise_x(0)
+        transpose_x(1, nc.scalar.copy)
+        group_w2()
+        first_matmul(0, vector_planes=(1, 3))
+        broadcast_vectors()
+        quantise_x(1)
+        transpose_x(2, nc.vector.tensor_copy)
+        regroup_h(0, nc.vector.tensor_copy)
+        first_matmul(1)
+        quantise_h(0)
+        for j in range(CHUNK_TILES[0]):
+            add_bias_to_x(0, j)
+        quantise_w2()
+        quantise_x(2)
+        transpose_x(3, nc.scalar.copy)
+        for k in range(N_CHUNKS + 1):
             step(k)

@@ -21,6 +21,7 @@ CHUNK_TILES = [2] + [4] * 15 + [2]
 N_CHUNKS = len(CHUNK_TILES)
 FIRST_TILE = [sum(CHUNK_TILES[:c]) for c in range(N_CHUNKS)]
 EPS = 1e-6
+OFFLOADED_TILES = 1
 
 FLOPS = 2 * TOKENS * D * F * 2
 
@@ -59,11 +60,11 @@ def tile_decoderlayer_pb_t_kernel(tc, h_attn, w1, b1, w2, b2, g2, be2, out):
         b1_bf = const.tile([P, PACK], BF16)
         with nc.allow_non_contiguous_dma(reason="four bias values to a partition"):
             nc.sync.dma_start(out=b1_bf[:], in_=b1.rearrange("(p m) -> p m", m=PACK))
-        nc.sync.dma_start(out=x_of(1), in_=rows_of(x_flat, 1))
         vec_rows = const.tile([P, 3, D], BF16)
         nc.vector.memset(vec_rows[:], 0.0)
         for i, vec in enumerate((b2, g2, be2)):
             nc.sync.dma_start(out=vec_rows[0:1, i, :], in_=vec.unsqueeze(0))
+        nc.sync.dma_start(out=x_of(1), in_=rows_of(x_flat, 1))
         raw_w2 = const.tile([P, PACK, D], BF16)
         nc.sync.dma_start(out=raw_w2[:], in_=w2.rearrange("(p t) d -> p t d", t=PACK))
         for c in range(2, N_CHUNKS):
@@ -97,26 +98,23 @@ def tile_decoderlayer_pb_t_kernel(tc, h_attn, w1, b1, w2, b2, g2, be2, out):
         w2_codes = const.tile([P, D], U32, align_bytes=64)
         w2_scales = const.tile([P, D], U8, align_bytes=64)
         b2_all = const.tile([P, D], BF16)
+        be2_all = const.tile([P, D], BF16)
         gain_shift = const_psum.tile([P, 2, D], BF16)
 
-        def group_w2():
-            nc.gpsimd.tensor_scalar(
-                out=grouped_w2[:],
-                in0=raw_w2[:].rearrange("p t d -> p d t"),
-                scalar1=1.0,
-                scalar2=0.0,
-                op0=ALU.mult,
-                op1=ALU.add,
-            )
+        def group_w2(copy):
+            copy(out=grouped_w2[:], in_=raw_w2[:].rearrange("p t d -> p d t"))
 
-        def broadcast_vectors():
+        def broadcast_b2():
             b2_ps = y_psum.tile([P, D], BF16, tag="y_ps")
             nc.tensor.matmul(out=b2_ps[:], lhsT=ones[:], rhs=vec_rows[:, 0, :], start=True, stop=True)
             nc.scalar.copy(out=b2_all[:], in_=b2_ps[:])
+
+        def broadcast_gain_and_shift():
             for i in range(2):
                 nc.tensor.matmul(
                     out=gain_shift[:, i, :], lhsT=ones[:], rhs=vec_rows[:, 1 + i, :], start=True, stop=True
                 )
+            nc.scalar.copy(out=be2_all[:], in_=gain_shift[:, 1, :])
 
         def quantise_w2():
             nc.vector.quantize_mx(
@@ -204,13 +202,15 @@ def tile_decoderlayer_pb_t_kernel(tc, h_attn, w1, b1, w2, b2, g2, be2, out):
                     )
             h_planes_of[c] = h_planes
 
-        def regroup_h(c, copy):
+        def start_regroup(c):
             grouped_h = work.tile([P, CHUNK_TILES[c] * P, PACK], BF16, align_bytes=64)
-            copy(
-                out=grouped_h[:].rearrange("p (c i) t -> p c t i", i=4),
-                in_=h_planes_of[c][:].rearrange("p t (c i) -> p c t i", i=4),
-            )
             grouped_h_of[c] = grouped_h
+
+        def regroup_h(c, copy, first, last):
+            copy(
+                out=grouped_h_of[c][:, first:last, :].rearrange("p (c i) t -> p c t i", i=4),
+                in_=h_planes_of[c][:, :, first:last].rearrange("p t (c i) -> p c t i", i=4),
+            )
 
         def add_bias_to_x(c, j):
             xb = per_tile.tile([P, D], F32)
@@ -275,46 +275,60 @@ def tile_decoderlayer_pb_t_kernel(tc, h_attn, w1, b1, w2, b2, g2, be2, out):
                 out=rstd[:, j0:j1], in_=sq_sum[:, j0:j1], func=ACT.Abs_reciprocal_sqrt, bias=eps_tile[:], scale=1.0 / D
             )
 
-        def shift_and_store(c):
-            for j in range(CHUNK_TILES[c]):
-                result = per_tile.tile([P, D], F32)
-                nc.vector.scalar_tensor_tensor(
-                    out=result[:],
-                    in0=scaled_of[c][:, j, :],
-                    scalar=rstd_of[c][:, j : j + 1],
-                    in1=gain_shift[:, 1, :],
-                    op0=ALU.mult,
-                    op1=ALU.add,
-                )
-                nc.sync.dma_start(out=rows_of(out_flat, c)[:, j, :], in_=result[:])
+        def shift_and_store(c, j):
+            result = per_tile.tile([P, D], F32)
+            nc.vector.scalar_tensor_tensor(
+                out=result[:],
+                in0=scaled_of[c][:, j, :],
+                scalar=rstd_of[c][:, j : j + 1],
+                in1=gain_shift[:, 1, :],
+                op0=ALU.mult,
+                op1=ALU.add,
+            )
+            nc.sync.dma_start(out=rows_of(out_flat, c)[:, j, :], in_=result[:])
+
+        def scale_shift_and_store(c, j):
+            normed = per_tile.tile([P, D], F32, tag="normed", bufs=2)
+            nc.scalar.activation(
+                out=normed[:], in_=scaled_of[c][:, j, :], func=ACT.Copy, scale=rstd_of[c][:, j : j + 1]
+            )
+            shifted = per_tile.tile([P, D], F32, tag="shifted", bufs=3)
+            nc.gpsimd.tensor_tensor(out=shifted[:], in0=normed[:], in1=be2_all[:], op=ALU.add)
+            nc.sync.dma_start(out=rows_of(out_flat, c)[:, j, :], in_=shifted[:])
+
+        def offloaded(c):
+            return OFFLOADED_TILES if CHUNK_TILES[c] == 4 else 0
 
         def step(k):
             has_residual = k < N_CHUNKS
             tiles = CHUNK_TILES[k] if has_residual else 0
             next_tiles = CHUNK_TILES[k + 1] if k + 1 < N_CHUNKS else 0
-            copy = nc.vector.tensor_copy if k == 0 else nc.scalar.copy
+            before = 2 if k > 0 else 0
             if has_residual:
                 start_residual(k)
-            for j in range(max(tiles, min(next_tiles, 2))):
+            for j in range(max(tiles, min(next_tiles, before))):
                 if j < tiles:
                     second_matmul(k, j)
-                if j < min(next_tiles, 2):
+                if j < min(next_tiles, before):
                     add_bias_to_x(k + 1, j)
             if has_residual:
                 negate_mean(k)
-            for j in range(2, next_tiles):
+            for j in range(before, next_tiles):
                 add_bias_to_x(k + 1, j)
             if k + 1 < N_CHUNKS:
-                regroup_h(k + 1, copy)
+                width = CHUNK_TILES[k + 1] * P
+                start_regroup(k + 1)
+                regroup_h(k + 1, nc.scalar.copy, 0, width)
             if k >= 1:
-                shift_and_store(k - 1)
+                for j in range(CHUNK_TILES[k - 1] - offloaded(k - 1)):
+                    shift_and_store(k - 1, j)
             if k + 2 < N_CHUNKS:
                 first_matmul(k + 2)
             if has_residual:
                 scaled = work.tile([P, tiles, D], F32)
                 scaled_of[k] = scaled
-                gain(k, 0)
-                gain(k, 1)
+                for j in range(min(tiles, 2)):
+                    gain(k, j)
             if k + 1 < N_CHUNKS:
                 quantise_h(k + 1)
             if k + 3 < N_CHUNKS:
@@ -329,26 +343,31 @@ def tile_decoderlayer_pb_t_kernel(tc, h_attn, w1, b1, w2, b2, g2, be2, out):
                     square(k, j, squares, sq_sum)
                     if k == N_CHUNKS - 1:
                         deviation(rstd, sq_sum, j, j + 1)
+            if k >= 1:
+                for j in range(CHUNK_TILES[k - 1] - offloaded(k - 1), CHUNK_TILES[k - 1]):
+                    scale_shift_and_store(k - 1, j)
             if k + 4 < N_CHUNKS:
-                transpose_x(k + 4, copy)
+                transpose_x(k + 4, nc.vector.tensor_copy if k == 0 else nc.scalar.copy)
             if has_residual:
                 if k < N_CHUNKS - 1:
                     deviation(rstd, sq_sum, 0, tiles)
                 rstd_of[k] = rstd
 
         transpose_x(0, nc.scalar.copy)
+        broadcast_b2()
         quantise_x(0)
-        transpose_x(1, nc.scalar.copy)
-        group_w2()
-        first_matmul(0, vector_planes=(1, 3))
-        broadcast_vectors()
-        quantise_x(1)
-        transpose_x(2, nc.vector.tensor_copy)
-        regroup_h(0, nc.vector.tensor_copy)
-        first_matmul(1)
-        quantise_h(0)
+        transpose_x(1, nc.vector.tensor_copy)
         for j in range(CHUNK_TILES[0]):
             add_bias_to_x(0, j)
+        first_matmul(0)
+        quantise_x(1)
+        start_regroup(0)
+        regroup_h(0, nc.scalar.copy, 0, CHUNK_TILES[0] * P)
+        broadcast_gain_and_shift()
+        transpose_x(2, nc.vector.tensor_copy)
+        quantise_h(0)
+        first_matmul(1)
+        group_w2(nc.vector.tensor_copy)
         quantise_w2()
         quantise_x(2)
         transpose_x(3, nc.scalar.copy)

@@ -22,6 +22,7 @@ N_CHUNKS = len(CHUNK_TILES)
 FIRST_TILE = [sum(CHUNK_TILES[:c]) for c in range(N_CHUNKS)]
 EPS = 1e-6
 OFFLOADED_TILES = 1
+GPSIMD_TOKENS = 128
 
 FLOPS = 2 * TOKENS * D * F * 2
 
@@ -125,6 +126,7 @@ def tile_decoderlayer_pb_t_kernel(tc, h_attn, w1, b1, w2, b2, g2, be2, out):
 
         grouped_x_of = {}
         x_mx_of = {}
+        h_ps_of = {}
         h_planes_of = {}
         grouped_h_of = {}
         h_mx_of = {}
@@ -172,12 +174,11 @@ def tile_decoderlayer_pb_t_kernel(tc, h_attn, w1, b1, w2, b2, g2, be2, out):
         def quantise_h(c):
             h_mx_of[c] = quantise(grouped_h_of[c], c)
 
-        def first_matmul(c, vector_planes=()):
+        def first_matmul(c):
             x_codes, x_scales = x_mx_of[c]
-            width = CHUNK_TILES[c] * P
-            h_planes = work.tile([P, PACK, width], BF16)
+            h_ps_of[c] = []
             for m in range(PACK):
-                h_ps = front_psum.tile([P, width], F32, tag="front")
+                h_ps = front_psum.tile([P, CHUNK_TILES[c] * P], F32, tag="front")
                 nc.tensor.matmul_mx(
                     out=h_ps[:],
                     lhsT=w1_codes[:, m * P : (m + 1) * P].bitcast(FP8X4),
@@ -187,19 +188,14 @@ def tile_decoderlayer_pb_t_kernel(tc, h_attn, w1, b1, w2, b2, g2, be2, out):
                     start=True,
                     stop=True,
                 )
-                if m in vector_planes:
-                    nc.vector.tensor_scalar(
-                        out=h_planes[:, m, :],
-                        in0=h_ps[:],
-                        scalar1=b1_cols[:, m : m + 1],
-                        scalar2=0.0,
-                        op0=ALU.add,
-                        op1=ALU.max,
-                    )
-                else:
-                    nc.scalar.activation(
-                        out=h_planes[:, m, :], in_=h_ps[:], func=ACT.Relu, bias=b1_cols[:, m : m + 1], scale=1.0
-                    )
+                h_ps_of[c].append(h_ps)
+
+        def relu(c):
+            h_planes = work.tile([P, PACK, CHUNK_TILES[c] * P], BF16)
+            for m in range(PACK):
+                nc.scalar.activation(
+                    out=h_planes[:, m, :], in_=h_ps_of[c][m][:], func=ACT.Relu, bias=b1_cols[:, m : m + 1], scale=1.0
+                )
             h_planes_of[c] = h_planes
 
         def start_regroup(c):
@@ -210,6 +206,16 @@ def tile_decoderlayer_pb_t_kernel(tc, h_attn, w1, b1, w2, b2, g2, be2, out):
             copy(
                 out=grouped_h_of[c][:, first:last, :].rearrange("p (c i) t -> p c t i", i=4),
                 in_=h_planes_of[c][:, :, first:last].rearrange("p t (c i) -> p c t i", i=4),
+            )
+
+        def regroup_h_on_gpsimd(c, first, last):
+            nc.gpsimd.tensor_scalar(
+                out=grouped_h_of[c][:, first:last, :],
+                in0=h_planes_of[c][:, :, first:last].rearrange("p t c -> p c t"),
+                scalar1=1.0,
+                scalar2=0.0,
+                op0=ALU.mult,
+                op1=ALU.add,
             )
 
         def add_bias_to_x(c, j):
@@ -289,8 +295,13 @@ def tile_decoderlayer_pb_t_kernel(tc, h_attn, w1, b1, w2, b2, g2, be2, out):
 
         def scale_shift_and_store(c, j):
             normed = per_tile.tile([P, D], F32, tag="normed", bufs=2)
-            nc.scalar.activation(
-                out=normed[:], in_=scaled_of[c][:, j, :], func=ACT.Copy, scale=rstd_of[c][:, j : j + 1]
+            nc.gpsimd.tensor_scalar(
+                out=normed[:],
+                in0=scaled_of[c][:, j, :],
+                scalar1=rstd_of[c][:, j : j + 1],
+                scalar2=0.0,
+                op0=ALU.mult,
+                op1=ALU.add,
             )
             shifted = per_tile.tile([P, D], F32, tag="shifted", bufs=3)
             nc.gpsimd.tensor_tensor(out=shifted[:], in0=normed[:], in1=be2_all[:], op=ALU.add)
@@ -298,6 +309,9 @@ def tile_decoderlayer_pb_t_kernel(tc, h_attn, w1, b1, w2, b2, g2, be2, out):
 
         def offloaded(c):
             return OFFLOADED_TILES if CHUNK_TILES[c] == 4 else 0
+
+        def gpsimd_tokens(c):
+            return GPSIMD_TOKENS if c >= 2 and CHUNK_TILES[c] == 4 else 0
 
         def step(k):
             has_residual = k < N_CHUNKS
@@ -307,23 +321,31 @@ def tile_decoderlayer_pb_t_kernel(tc, h_attn, w1, b1, w2, b2, g2, be2, out):
             if has_residual:
                 start_residual(k)
             for j in range(max(tiles, min(next_tiles, before))):
+                if j == min(tiles, 3) and k + 2 < N_CHUNKS:
+                    first_matmul(k + 2)
                 if j < tiles:
                     second_matmul(k, j)
                 if j < min(next_tiles, before):
                     add_bias_to_x(k + 1, j)
+            if k + 2 < N_CHUNKS and k + 2 not in h_ps_of:
+                first_matmul(k + 2)
             if has_residual:
                 negate_mean(k)
             for j in range(before, next_tiles):
                 add_bias_to_x(k + 1, j)
             if k + 1 < N_CHUNKS:
                 width = CHUNK_TILES[k + 1] * P
-                start_regroup(k + 1)
-                regroup_h(k + 1, nc.scalar.copy, 0, width)
+                if k + 1 < 2:
+                    start_regroup(k + 1)
+                regroup_h(k + 1, nc.scalar.copy, gpsimd_tokens(k + 1), width)
             if k >= 1:
                 for j in range(CHUNK_TILES[k - 1] - offloaded(k - 1)):
                     shift_and_store(k - 1, j)
             if k + 2 < N_CHUNKS:
-                first_matmul(k + 2)
+                relu(k + 2)
+                start_regroup(k + 2)
+                if gpsimd_tokens(k + 2) > 0:
+                    regroup_h_on_gpsimd(k + 2, 0, gpsimd_tokens(k + 2))
             if has_residual:
                 scaled = work.tile([P, tiles, D], F32)
                 scaled_of[k] = scaled
@@ -360,6 +382,7 @@ def tile_decoderlayer_pb_t_kernel(tc, h_attn, w1, b1, w2, b2, g2, be2, out):
         for j in range(CHUNK_TILES[0]):
             add_bias_to_x(0, j)
         first_matmul(0)
+        relu(0)
         quantise_x(1)
         start_regroup(0)
         regroup_h(0, nc.scalar.copy, 0, CHUNK_TILES[0] * P)
@@ -367,6 +390,7 @@ def tile_decoderlayer_pb_t_kernel(tc, h_attn, w1, b1, w2, b2, g2, be2, out):
         transpose_x(2, nc.vector.tensor_copy)
         quantise_h(0)
         first_matmul(1)
+        relu(1)
         group_w2(nc.vector.tensor_copy)
         quantise_w2()
         quantise_x(2)

@@ -21,8 +21,7 @@ CHUNK_TILES = [2] + [4] * 15 + [2]
 N_CHUNKS = len(CHUNK_TILES)
 FIRST_TILE = [sum(CHUNK_TILES[:c]) for c in range(N_CHUNKS)]
 EPS = 1e-6
-OFFLOADED_TILES = 1
-GPSIMD_TOKENS = 128
+GPSIMD_TOKENS = 192
 
 FLOPS = 2 * TOKENS * D * F * 2
 
@@ -253,7 +252,8 @@ def tile_decoderlayer_pb_t_kernel(tc, h_attn, w1, b1, w2, b2, g2, be2, out):
 
         def negate_mean(c):
             neg_mean = small.tile([P, CHUNK_TILES[c]], F32)
-            nc.gpsimd.tensor_scalar_mul(out=neg_mean[:], in0=r_sum_of[c][:], scalar1=-1.0 / D)
+            engine = nc.vector if c >= N_CHUNKS - 2 else nc.gpsimd
+            engine.tensor_scalar_mul(out=neg_mean[:], in0=r_sum_of[c][:], scalar1=-1.0 / D)
             neg_mean_of[c] = neg_mean
 
         def gain(c, j):
@@ -295,20 +295,15 @@ def tile_decoderlayer_pb_t_kernel(tc, h_attn, w1, b1, w2, b2, g2, be2, out):
 
         def scale_shift_and_store(c, j):
             normed = per_tile.tile([P, D], F32, tag="normed", bufs=2)
-            nc.gpsimd.tensor_scalar(
-                out=normed[:],
-                in0=scaled_of[c][:, j, :],
-                scalar1=rstd_of[c][:, j : j + 1],
-                scalar2=0.0,
-                op0=ALU.mult,
-                op1=ALU.add,
+            nc.scalar.activation(
+                out=normed[:], in_=scaled_of[c][:, j, :], func=ACT.Copy, scale=rstd_of[c][:, j : j + 1]
             )
             shifted = per_tile.tile([P, D], F32, tag="shifted", bufs=3)
             nc.gpsimd.tensor_tensor(out=shifted[:], in0=normed[:], in1=be2_all[:], op=ALU.add)
             nc.sync.dma_start(out=rows_of(out_flat, c)[:, j, :], in_=shifted[:])
 
         def offloaded(c):
-            return OFFLOADED_TILES if CHUNK_TILES[c] == 4 else 0
+            return 1 + max(0, c - (N_CHUNKS - 4)) if CHUNK_TILES[c] == 4 else 0
 
         def gpsimd_tokens(c):
             return GPSIMD_TOKENS if c >= 2 and CHUNK_TILES[c] == 4 else 0
@@ -318,6 +313,9 @@ def tile_decoderlayer_pb_t_kernel(tc, h_attn, w1, b1, w2, b2, g2, be2, out):
             tiles = CHUNK_TILES[k] if has_residual else 0
             next_tiles = CHUNK_TILES[k + 1] if k + 1 < N_CHUNKS else 0
             before = 2 if k > 0 else 0
+            if k >= N_CHUNKS - 2:
+                for j in range(CHUNK_TILES[k - 1] - offloaded(k - 1), CHUNK_TILES[k - 1]):
+                    scale_shift_and_store(k - 1, j)
             if has_residual:
                 start_residual(k)
             for j in range(max(tiles, min(next_tiles, before))):
@@ -349,14 +347,14 @@ def tile_decoderlayer_pb_t_kernel(tc, h_attn, w1, b1, w2, b2, g2, be2, out):
             if has_residual:
                 scaled = work.tile([P, tiles, D], F32)
                 scaled_of[k] = scaled
-                for j in range(min(tiles, 2)):
+                for j in range(min(tiles, 3)):
                     gain(k, j)
             if k + 1 < N_CHUNKS:
                 quantise_h(k + 1)
             if k + 3 < N_CHUNKS:
                 quantise_x(k + 3)
             if has_residual:
-                for j in range(2, tiles):
+                for j in range(3, tiles):
                     gain(k, j)
                 squares = work.tile([P, tiles, D], BF16)
                 sq_sum = small.tile([P, tiles], F32)
@@ -365,7 +363,7 @@ def tile_decoderlayer_pb_t_kernel(tc, h_attn, w1, b1, w2, b2, g2, be2, out):
                     square(k, j, squares, sq_sum)
                     if k == N_CHUNKS - 1:
                         deviation(rstd, sq_sum, j, j + 1)
-            if k >= 1:
+            if 1 <= k < N_CHUNKS - 2:
                 for j in range(CHUNK_TILES[k - 1] - offloaded(k - 1), CHUNK_TILES[k - 1]):
                     scale_shift_and_store(k - 1, j)
             if k + 4 < N_CHUNKS:

@@ -21,7 +21,8 @@ CHUNK_TILES = [2] + [4] * 15 + [2]
 N_CHUNKS = len(CHUNK_TILES)
 FIRST_TILE = [sum(CHUNK_TILES[:c]) for c in range(N_CHUNKS)]
 EPS = 1e-6
-GPSIMD_TOKENS = 192
+OFFLOADED_TILES = 1
+GPSIMD_TOKENS = 128
 
 FLOPS = 2 * TOKENS * D * F * 2
 
@@ -242,9 +243,9 @@ def tile_decoderlayer_pb_t_kernel(tc, h_attn, w1, b1, w2, b2, g2, be2, out):
             )
             nc.vector.scalar_tensor_tensor(
                 out=r_of[c][:, j, :],
-                in0=y_ps[:],
+                in0=xb_of[(c, j)][:],
                 scalar=0.0,
-                in1=xb_of[(c, j)][:],
+                in1=y_ps[:],
                 op0=ALU.add,
                 op1=ALU.add,
                 accum_out=r_sum_of[c][:, j : j + 1],
@@ -252,8 +253,7 @@ def tile_decoderlayer_pb_t_kernel(tc, h_attn, w1, b1, w2, b2, g2, be2, out):
 
         def negate_mean(c):
             neg_mean = small.tile([P, CHUNK_TILES[c]], F32)
-            engine = nc.vector if c >= N_CHUNKS - 2 else nc.gpsimd
-            engine.tensor_scalar_mul(out=neg_mean[:], in0=r_sum_of[c][:], scalar1=-1.0 / D)
+            nc.vector.tensor_scalar_mul(out=neg_mean[:], in0=r_sum_of[c][:], scalar1=-1.0 / D)
             neg_mean_of[c] = neg_mean
 
         def gain(c, j):
@@ -303,7 +303,7 @@ def tile_decoderlayer_pb_t_kernel(tc, h_attn, w1, b1, w2, b2, g2, be2, out):
             nc.sync.dma_start(out=rows_of(out_flat, c)[:, j, :], in_=shifted[:])
 
         def offloaded(c):
-            return 1 + max(0, c - (N_CHUNKS - 4)) if CHUNK_TILES[c] == 4 else 0
+            return OFFLOADED_TILES if CHUNK_TILES[c] == 4 else 0
 
         def gpsimd_tokens(c):
             return GPSIMD_TOKENS if c >= 2 and CHUNK_TILES[c] == 4 else 0
@@ -312,23 +312,19 @@ def tile_decoderlayer_pb_t_kernel(tc, h_attn, w1, b1, w2, b2, g2, be2, out):
             has_residual = k < N_CHUNKS
             tiles = CHUNK_TILES[k] if has_residual else 0
             next_tiles = CHUNK_TILES[k + 1] if k + 1 < N_CHUNKS else 0
-            before = 2 if k > 0 else 0
-            if k >= N_CHUNKS - 2:
+            before = tiles
+            if k >= N_CHUNKS - 0:
                 for j in range(CHUNK_TILES[k - 1] - offloaded(k - 1), CHUNK_TILES[k - 1]):
                     scale_shift_and_store(k - 1, j)
             if has_residual:
                 start_residual(k)
             for j in range(max(tiles, min(next_tiles, before))):
-                if j == min(tiles, 3) and k + 2 < N_CHUNKS:
-                    first_matmul(k + 2)
                 if j < tiles:
                     second_matmul(k, j)
                 if j < min(next_tiles, before):
                     add_bias_to_x(k + 1, j)
             if k + 2 < N_CHUNKS and k + 2 not in h_ps_of:
                 first_matmul(k + 2)
-            if has_residual:
-                negate_mean(k)
             for j in range(before, next_tiles):
                 add_bias_to_x(k + 1, j)
             if k + 1 < N_CHUNKS:
@@ -338,7 +334,11 @@ def tile_decoderlayer_pb_t_kernel(tc, h_attn, w1, b1, w2, b2, g2, be2, out):
                 regroup_h(k + 1, nc.scalar.copy, gpsimd_tokens(k + 1), width)
             if k >= 1:
                 for j in range(CHUNK_TILES[k - 1] - offloaded(k - 1)):
+                    if j == 1 and has_residual:
+                        negate_mean(k)
                     shift_and_store(k - 1, j)
+            if has_residual and k not in neg_mean_of:
+                negate_mean(k)
             if k + 2 < N_CHUNKS:
                 relu(k + 2)
                 start_regroup(k + 2)
@@ -363,7 +363,7 @@ def tile_decoderlayer_pb_t_kernel(tc, h_attn, w1, b1, w2, b2, g2, be2, out):
                     square(k, j, squares, sq_sum)
                     if k == N_CHUNKS - 1:
                         deviation(rstd, sq_sum, j, j + 1)
-            if 1 <= k < N_CHUNKS - 2:
+            if 1 <= k < N_CHUNKS - 0:
                 for j in range(CHUNK_TILES[k - 1] - offloaded(k - 1), CHUNK_TILES[k - 1]):
                     scale_shift_and_store(k - 1, j)
             if k + 4 < N_CHUNKS:

@@ -19,10 +19,9 @@ F = 512
 TILES = TOKENS // P
 CHUNK_TILES = [2] + [4] * 15 + [2]
 N_CHUNKS = len(CHUNK_TILES)
+LAST = N_CHUNKS - 1
 FIRST_TILE = [sum(CHUNK_TILES[:c]) for c in range(N_CHUNKS)]
 EPS = 1e-6
-OFFLOADED_TILES = 1
-GPSIMD_TOKENS = 128
 
 FLOPS = 2 * TOKENS * D * F * 2
 
@@ -115,7 +114,6 @@ def tile_decoderlayer_pb_t_kernel(tc, h_attn, w1, b1, w2, b2, g2, be2, out):
                 nc.tensor.matmul(
                     out=gain_shift[:, i, :], lhsT=ones[:], rhs=vec_rows[:, 1 + i, :], start=True, stop=True
                 )
-            nc.scalar.copy(out=be2_all[:], in_=gain_shift[:, 1, :])
 
         def quantise_w2():
             nc.vector.quantize_mx(
@@ -124,12 +122,10 @@ def tile_decoderlayer_pb_t_kernel(tc, h_attn, w1, b1, w2, b2, g2, be2, out):
                 in_=grouped_w2[:].rearrange("p c t -> p (c t)"),
             )
 
-        grouped_x_of = {}
-        x_mx_of = {}
+        grouped_of = {}
+        mx_of = {}
         h_ps_of = {}
         h_planes_of = {}
-        grouped_h_of = {}
-        h_mx_of = {}
         xb_of = {}
         r_of = {}
         r_sum_of = {}
@@ -137,11 +133,34 @@ def tile_decoderlayer_pb_t_kernel(tc, h_attn, w1, b1, w2, b2, g2, be2, out):
         scaled_of = {}
         rstd_of = {}
 
+        def width_of(c):
+            return CHUNK_TILES[c] * P if 0 <= c < N_CHUNKS else 0
+
+        def start_group(k, h_width, x_width):
+            grouped = work.tile([P, h_width + x_width, PACK], BF16, align_bytes=64)
+            grouped_of[k] = grouped
+
+        def x_slot(c):
+            first = width_of(c - 2)
+            return c - 3, first, first + width_of(c)
+
+        def h_slot(c):
+            return c - 1, 0, width_of(c)
+
+        def quantise(k, first, last):
+            codes = work.tile([P, last - first], U32, align_bytes=64, tag="codes", bufs=5)
+            scales = work.tile([P, last - first], U8, align_bytes=64, tag="scales", bufs=5)
+            nc.vector.quantize_mx(
+                out=codes[:].bitcast(FP8X4),
+                scales=scales[:],
+                in_=grouped_of[k][:, first:last, :].rearrange("p c t -> p (c t)"),
+            )
+            return codes, scales
+
         def transpose_x(c, copy):
             x_words = x_of(c).bitcast(F32)
-            width = CHUNK_TILES[c] * P
-            grouped_x = work.tile([P, width, PACK], BF16, align_bytes=64)
-            gx_words = grouped_x[:].bitcast(F32)
+            k, first, last = x_slot(c)
+            gx_words = grouped_of[k][:, first:last, :].bitcast(F32)
             pairs = CHUNK_TILES[c] // 2
             banks = []
             for pair in range(pairs):
@@ -157,65 +176,37 @@ def tile_decoderlayer_pb_t_kernel(tc, h_attn, w1, b1, w2, b2, g2, be2, out):
                     out=gx_words[:, 2 * P * pair : 2 * P * (pair + 1), :].rearrange("p (jj r) u -> p jj r u", jj=2),
                     in_=banks[pair][:].rearrange("p jj u r -> p jj r u"),
                 )
-            grouped_x_of[c] = grouped_x
-
-        def quantise(grouped, c):
-            width = CHUNK_TILES[c] * P
-            codes = work.tile([P, width], U32, align_bytes=64, tag="codes", bufs=4)
-            scales = work.tile([P, width], U8, align_bytes=64, tag="scales", bufs=4)
-            nc.vector.quantize_mx(
-                out=codes[:].bitcast(FP8X4), scales=scales[:], in_=grouped[:].rearrange("p c t -> p (c t)")
-            )
-            return codes, scales
-
-        def quantise_x(c):
-            x_mx_of[c] = quantise(grouped_x_of[c], c)
-
-        def quantise_h(c):
-            h_mx_of[c] = quantise(grouped_h_of[c], c)
 
         def first_matmul(c):
-            x_codes, x_scales = x_mx_of[c]
+            codes, scales, first = mx_of[("x", c)]
+            words = slice(first, first + width_of(c))
             h_ps_of[c] = []
             for m in range(PACK):
-                h_ps = front_psum.tile([P, CHUNK_TILES[c] * P], F32, tag="front")
+                h_ps = front_psum.tile([P, width_of(c)], F32, tag="front")
                 nc.tensor.matmul_mx(
                     out=h_ps[:],
                     lhsT=w1_codes[:, m * P : (m + 1) * P].bitcast(FP8X4),
                     lhsT_scale=w1_scales[:, m * P : (m + 1) * P],
-                    rhs=x_codes[:].bitcast(FP8X4),
-                    rhs_scale=x_scales[:],
+                    rhs=codes[:, words].bitcast(FP8X4),
+                    rhs_scale=scales[:, words],
                     start=True,
                     stop=True,
                 )
                 h_ps_of[c].append(h_ps)
 
         def relu(c):
-            h_planes = work.tile([P, PACK, CHUNK_TILES[c] * P], BF16)
+            h_planes = work.tile([P, PACK, width_of(c)], BF16)
             for m in range(PACK):
                 nc.scalar.activation(
                     out=h_planes[:, m, :], in_=h_ps_of[c][m][:], func=ACT.Relu, bias=b1_cols[:, m : m + 1], scale=1.0
                 )
             h_planes_of[c] = h_planes
 
-        def start_regroup(c):
-            grouped_h = work.tile([P, CHUNK_TILES[c] * P, PACK], BF16, align_bytes=64)
-            grouped_h_of[c] = grouped_h
-
-        def regroup_h(c, copy, first, last):
+        def regroup_h(c, copy):
+            k, first, last = h_slot(c)
             copy(
-                out=grouped_h_of[c][:, first:last, :].rearrange("p (c i) t -> p c t i", i=4),
-                in_=h_planes_of[c][:, :, first:last].rearrange("p t (c i) -> p c t i", i=4),
-            )
-
-        def regroup_h_on_gpsimd(c, first, last):
-            nc.gpsimd.tensor_scalar(
-                out=grouped_h_of[c][:, first:last, :],
-                in0=h_planes_of[c][:, :, first:last].rearrange("p t c -> p c t"),
-                scalar1=1.0,
-                scalar2=0.0,
-                op0=ALU.mult,
-                op1=ALU.add,
+                out=grouped_of[k][:, first:last, :].rearrange("p (c i) t -> p c t i", i=4),
+                in_=h_planes_of[c][:].rearrange("p t (c i) -> p c t i", i=4),
             )
 
         def add_bias_to_x(c, j):
@@ -230,12 +221,13 @@ def tile_decoderlayer_pb_t_kernel(tc, h_attn, w1, b1, w2, b2, g2, be2, out):
             r_sum_of[c] = r_sum
 
         def second_matmul(c, j):
-            h_codes, h_scales = h_mx_of[c]
+            codes, scales, first = mx_of[("h", c)]
+            words = slice(first + j * P, first + (j + 1) * P)
             y_ps = y_psum.tile([P, D], F32)
             nc.tensor.matmul_mx(
                 out=y_ps[:],
-                lhsT=h_codes[:, j * P : (j + 1) * P].bitcast(FP8X4),
-                lhsT_scale=h_scales[:, j * P : (j + 1) * P],
+                lhsT=codes[:, words].bitcast(FP8X4),
+                lhsT_scale=scales[:, words],
                 rhs=w2_codes[:].bitcast(FP8X4),
                 rhs_scale=w2_scales[:],
                 start=True,
@@ -243,17 +235,17 @@ def tile_decoderlayer_pb_t_kernel(tc, h_attn, w1, b1, w2, b2, g2, be2, out):
             )
             nc.vector.scalar_tensor_tensor(
                 out=r_of[c][:, j, :],
-                in0=xb_of[(c, j)][:],
+                in0=y_ps[:],
                 scalar=0.0,
-                in1=y_ps[:],
+                in1=xb_of[(c, j)][:],
                 op0=ALU.add,
                 op1=ALU.add,
                 accum_out=r_sum_of[c][:, j : j + 1],
             )
 
-        def negate_mean(c):
+        def negate_mean(c, engine):
             neg_mean = small.tile([P, CHUNK_TILES[c]], F32)
-            nc.vector.tensor_scalar_mul(out=neg_mean[:], in0=r_sum_of[c][:], scalar1=-1.0 / D)
+            engine.tensor_scalar_mul(out=neg_mean[:], in0=r_sum_of[c][:], scalar1=-1.0 / D)
             neg_mean_of[c] = neg_mean
 
         def gain(c, j):
@@ -303,95 +295,101 @@ def tile_decoderlayer_pb_t_kernel(tc, h_attn, w1, b1, w2, b2, g2, be2, out):
             nc.sync.dma_start(out=rows_of(out_flat, c)[:, j, :], in_=shifted[:])
 
         def offloaded(c):
-            return OFFLOADED_TILES if CHUNK_TILES[c] == 4 else 0
+            return 1 + max(0, c - (LAST - 3)) if CHUNK_TILES[c] == 4 else 0
 
-        def gpsimd_tokens(c):
-            return GPSIMD_TOKENS if c >= 2 and CHUNK_TILES[c] == 4 else 0
+        def quantise_step(k):
+            h_width, x_width = width_of(k + 1), width_of(k + 3)
+            if h_width == x_width:
+                codes, scales = quantise(k, 0, h_width + x_width)
+                mx_of[("h", k + 1)] = (codes, scales, 0)
+                mx_of[("x", k + 3)] = (codes, scales, h_width)
+            else:
+                if h_width > 0:
+                    mx_of[("h", k + 1)] = quantise(k, 0, h_width) + (0,)
+                if x_width > 0:
+                    mx_of[("x", k + 3)] = quantise(k, h_width, h_width + x_width) + (0,)
 
         def step(k):
-            has_residual = k < N_CHUNKS
+            has_residual = k <= LAST
             tiles = CHUNK_TILES[k] if has_residual else 0
-            next_tiles = CHUNK_TILES[k + 1] if k + 1 < N_CHUNKS else 0
-            before = tiles
-            if k >= N_CHUNKS - 0:
+            next_tiles = CHUNK_TILES[k + 1] if k < LAST else 0
+            if k >= LAST - 1:
                 for j in range(CHUNK_TILES[k - 1] - offloaded(k - 1), CHUNK_TILES[k - 1]):
                     scale_shift_and_store(k - 1, j)
             if has_residual:
                 start_residual(k)
-            for j in range(max(tiles, min(next_tiles, before))):
+            ahead = 2 if k > 0 else 0
+            for j in range(max(tiles, min(next_tiles, ahead))):
                 if j < tiles:
                     second_matmul(k, j)
-                if j < min(next_tiles, before):
+                if j < min(next_tiles, ahead):
                     add_bias_to_x(k + 1, j)
-            if k + 2 < N_CHUNKS and k + 2 not in h_ps_of:
-                first_matmul(k + 2)
-            for j in range(before, next_tiles):
+            for j in range(ahead, next_tiles):
                 add_bias_to_x(k + 1, j)
-            if k + 1 < N_CHUNKS:
-                width = CHUNK_TILES[k + 1] * P
-                if k + 1 < 2:
-                    start_regroup(k + 1)
-                regroup_h(k + 1, nc.scalar.copy, gpsimd_tokens(k + 1), width)
+            if k < LAST:
+                regroup_h(k + 1, nc.scalar.copy)
             if k >= 1:
                 for j in range(CHUNK_TILES[k - 1] - offloaded(k - 1)):
-                    if j == 1 and has_residual:
-                        negate_mean(k)
                     shift_and_store(k - 1, j)
-            if has_residual and k not in neg_mean_of:
-                negate_mean(k)
-            if k + 2 < N_CHUNKS:
+                    if j == 0 and has_residual:
+                        negate_mean(k, nc.vector)
+            elif has_residual:
+                negate_mean(k, nc.vector)
+            if k + 2 <= LAST:
+                first_matmul(k + 2)
                 relu(k + 2)
-                start_regroup(k + 2)
-                if gpsimd_tokens(k + 2) > 0:
-                    regroup_h_on_gpsimd(k + 2, 0, gpsimd_tokens(k + 2))
             if has_residual:
                 scaled = work.tile([P, tiles, D], F32)
                 scaled_of[k] = scaled
-                for j in range(min(tiles, 3)):
+                for j in range(min(tiles, 2)):
                     gain(k, j)
-            if k + 1 < N_CHUNKS:
-                quantise_h(k + 1)
-            if k + 3 < N_CHUNKS:
-                quantise_x(k + 3)
+            if k < LAST:
+                quantise_step(k)
             if has_residual:
-                for j in range(3, tiles):
+                for j in range(2, tiles):
                     gain(k, j)
                 squares = work.tile([P, tiles, D], BF16)
                 sq_sum = small.tile([P, tiles], F32)
                 rstd = small.tile([P, tiles], F32)
                 for j in range(tiles):
                     square(k, j, squares, sq_sum)
-                    if k == N_CHUNKS - 1:
+                    if k == LAST:
                         deviation(rstd, sq_sum, j, j + 1)
-            if 1 <= k < N_CHUNKS - 0:
+            if 1 <= k < LAST - 1:
                 for j in range(CHUNK_TILES[k - 1] - offloaded(k - 1), CHUNK_TILES[k - 1]):
                     scale_shift_and_store(k - 1, j)
-            if k + 4 < N_CHUNKS:
+            if k + 2 <= LAST:
+                start_group(k + 1, width_of(k + 2), width_of(k + 4))
+            if k + 4 <= LAST:
                 transpose_x(k + 4, nc.vector.tensor_copy if k == 0 else nc.scalar.copy)
             if has_residual:
-                if k < N_CHUNKS - 1:
+                if k < LAST:
                     deviation(rstd, sq_sum, 0, tiles)
                 rstd_of[k] = rstd
 
+        start_group(-3, 0, width_of(0))
         transpose_x(0, nc.scalar.copy)
         broadcast_b2()
-        quantise_x(0)
+        mx_of[("x", 0)] = quantise(-3, 0, width_of(0)) + (0,)
+        start_group(-2, 0, width_of(1))
         transpose_x(1, nc.vector.tensor_copy)
         for j in range(CHUNK_TILES[0]):
             add_bias_to_x(0, j)
         first_matmul(0)
         relu(0)
-        quantise_x(1)
-        start_regroup(0)
-        regroup_h(0, nc.scalar.copy, 0, CHUNK_TILES[0] * P)
+        mx_of[("x", 1)] = quantise(-2, 0, width_of(1)) + (0,)
+        start_group(-1, width_of(0), width_of(2))
+        regroup_h(0, nc.scalar.copy)
         broadcast_gain_and_shift()
+        nc.scalar.copy(out=be2_all[:], in_=gain_shift[:, 1, :])
         transpose_x(2, nc.vector.tensor_copy)
-        quantise_h(0)
+        mx_of[("h", 0)] = quantise(-1, 0, width_of(0)) + (0,)
         first_matmul(1)
         relu(1)
         group_w2(nc.vector.tensor_copy)
         quantise_w2()
-        quantise_x(2)
+        mx_of[("x", 2)] = quantise(-1, width_of(0), width_of(0) + width_of(2)) + (0,)
+        start_group(0, width_of(1), width_of(3))
         transpose_x(3, nc.scalar.copy)
         for k in range(N_CHUNKS + 1):
             step(k)

from contextlib import ExitStack

import concourse.mybir as mybir
from concourse.masks import make_identity

F32 = mybir.dt.float32
BF16 = mybir.dt.bfloat16
U32 = mybir.dt.uint32
U8 = mybir.dt.uint8
FP8X4 = mybir.dt.float8_e4m3fn_x4
ACT = mybir.ActivationFunctionType
ALU = mybir.AluOpType

P = 128
PACK = 4
TOKENS = 8 * 1024
D = 512
F = 512
TILES = TOKENS // P
CHUNK_TILES = [2] + [4] * 15 + [2]
N_CHUNKS = len(CHUNK_TILES)
LAST = N_CHUNKS - 1
FIRST_TILE = [sum(CHUNK_TILES[:c]) for c in range(N_CHUNKS)]
EPS = 1e-6

FLOPS = 2 * TOKENS * D * F * 2


def tile_decoderlayer_pb_t_kernel(tc, h_attn, w1, b1, w2, b2, g2, be2, out):
    nc = tc.nc
    x_flat = h_attn.flatten_outer_dims()
    out_flat = out.flatten_outer_dims()

    def rows_of(flat, c):
        jn = CHUNK_TILES[c]
        first = FIRST_TILE[c] * P
        return flat[first : first + jn * P, :].rearrange("(p j) d -> p j d", j=jn)

    with ExitStack() as stack:
        const = stack.enter_context(tc.tile_pool(name="const", bufs=1))
        work = stack.enter_context(tc.tile_pool(name="work", bufs=2))
        per_tile = stack.enter_context(tc.tile_pool(name="per_tile", bufs=4))
        small = stack.enter_context(tc.tile_pool(name="small", bufs=3))
        const_psum = stack.enter_context(tc.psum_pool(name="const_psum", bufs=1))
        front_psum = stack.enter_context(tc.psum_pool(name="front_psum", bufs=4))
        y_psum = stack.enter_context(tc.psum_pool(name="y_psum", bufs=3))
        stack.enter_context(tc.manual_schedule())

        x_all = const.tile([P, TILES, D], BF16)

        def x_of(c):
            return x_all[:, FIRST_TILE[c] : FIRST_TILE[c] + CHUNK_TILES[c]]

        raw_w1 = const.tile([P, PACK, F], BF16)
        nc.sync.dma_start(
            out=raw_w1[:].rearrange("p (u e) f -> p u (e f)", u=2),
            in_=w1.rearrange("(u q e) f -> q u (e f)", u=2, e=2),
        )
        nc.sync.dma_start(out=x_of(0), in_=rows_of(x_flat, 0))
        b1_bf = const.tile([P, PACK], BF16)
        with nc.allow_non_contiguous_dma(reason="four bias values to a partition"):
            nc.sync.dma_start(out=b1_bf[:], in_=b1.rearrange("(p m) -> p m", m=PACK))
        vec_rows = const.tile([P, 3, D], BF16)
        nc.vector.memset(vec_rows[:], 0.0)
        for i, vec in enumerate((b2, g2, be2)):
            nc.sync.dma_start(out=vec_rows[0:1, i, :], in_=vec.unsqueeze(0))
        nc.sync.dma_start(out=x_of(1), in_=rows_of(x_flat, 1))
        raw_w2 = const.tile([P, PACK, D], BF16)
        nc.sync.dma_start(out=raw_w2[:], in_=w2.rearrange("(p t) d -> p t d", t=PACK))
        for c in range(2, N_CHUNKS):
            nc.sync.dma_start(out=x_of(c), in_=rows_of(x_flat, c))

        eps_tile = const.tile([P, 1], F32)
        nc.vector.memset(eps_tile[:], EPS)
        warm = const.tile([P, 1], F32)
        nc.scalar.activation(out=warm[:], in_=eps_tile[:], func=ACT.Abs_reciprocal_sqrt)
        ident = const.tile([P, P], F32)
        make_identity(nc, ident[:])
        ones = const.tile([P, P], BF16)
        nc.vector.memset(ones[:], 1.0)

        grouped_w1 = const.tile([P, F, PACK], BF16, align_bytes=64)
        w1_by_m = raw_w1[:].rearrange("p t (i m) -> p m i t", m=PACK)
        for m in range(PACK):
            w1_copy = nc.scalar.copy if m == 3 else nc.vector.tensor_copy
            w1_copy(out=grouped_w1[:, m * P : (m + 1) * P, :], in_=w1_by_m[:, m])
        w1_codes = const.tile([P, F], U32, align_bytes=64)
        w1_scales = const.tile([P, F], U8, align_bytes=64)
        nc.vector.quantize_mx(
            out=w1_codes[:].bitcast(FP8X4),
            scales=w1_scales[:],
            in_=grouped_w1[:].rearrange("p c t -> p (c t)"),
        )
        b1_cols = const.tile([P, PACK], F32)
        nc.gpsimd.tensor_copy(out=b1_cols[:], in_=b1_bf[:])

        grouped_w2 = const.tile([P, D, PACK], BF16, align_bytes=64)
        w2_codes = const.tile([P, D], U32, align_bytes=64)
        w2_scales = const.tile([P, D], U8, align_bytes=64)
        b2_all = const.tile([P, D], BF16)
        be2_all = const.tile([P, D], BF16)
        gain_shift = const_psum.tile([P, 2, D], BF16)

        def group_w2(copy):
            copy(out=grouped_w2[:], in_=raw_w2[:].rearrange("p t d -> p d t"))

        def broadcast_b2():
            b2_ps = y_psum.tile([P, D], BF16, tag="y_ps")
            nc.tensor.matmul(out=b2_ps[:], lhsT=ones[:], rhs=vec_rows[:, 0, :], start=True, stop=True)
            nc.scalar.copy(out=b2_all[:], in_=b2_ps[:])

        def broadcast_gain_and_shift():
            for i in range(2):
                nc.tensor.matmul(
                    out=gain_shift[:, i, :], lhsT=ones[:], rhs=vec_rows[:, 1 + i, :], start=True, stop=True
                )

        def quantise_w2():
            nc.vector.quantize_mx(
                out=w2_codes[:].bitcast(FP8X4),
                scales=w2_scales[:],
                in_=grouped_w2[:].rearrange("p c t -> p (c t)"),
            )

        grouped_of = {}
        mx_of = {}
        h_ps_of = {}
        h_planes_of = {}
        xb_of = {}
        r_of = {}
        r_sum_of = {}
        neg_mean_of = {}
        scaled_of = {}
        rstd_of = {}

        def width_of(c):
            return CHUNK_TILES[c] * P if 0 <= c < N_CHUNKS else 0

        def start_group(k, h_width, x_width):
            grouped = work.tile([P, h_width + x_width, PACK], BF16, align_bytes=64)
            grouped_of[k] = grouped

        def x_slot(c):
            first = width_of(c - 2)
            return c - 3, first, first + width_of(c)

        def h_slot(c):
            return c - 1, 0, width_of(c)

        def quantise(k, first, last):
            codes = work.tile([P, last - first], U32, align_bytes=64, tag="codes", bufs=5)
            scales = work.tile([P, last - first], U8, align_bytes=64, tag="scales", bufs=5)
            nc.vector.quantize_mx(
                out=codes[:].bitcast(FP8X4),
                scales=scales[:],
                in_=grouped_of[k][:, first:last, :].rearrange("p c t -> p (c t)"),
            )
            return codes, scales

        def transpose_x(c, copy):
            x_words = x_of(c).bitcast(F32)
            k, first, last = x_slot(c)
            gx_words = grouped_of[k][:, first:last, :].bitcast(F32)
            pairs = CHUNK_TILES[c] // 2
            banks = []
            for pair in range(pairs):
                xt = front_psum.tile([P, 2, 2, P], F32, tag="front")
                for jj in range(2):
                    for u in range(2):
                        nc.tensor.transpose(
                            xt[:, jj, u, :], x_words[:, 2 * pair + jj, u * P : (u + 1) * P], ident[:]
                        )
                banks.append(xt)
            for pair in range(pairs):
                copy(
                    out=gx_words[:, 2 * P * pair : 2 * P * (pair + 1), :].rearrange("p (jj r) u -> p jj r u", jj=2),
                    in_=banks[pair][:].rearrange("p jj u r -> p jj r u"),
                )

        def first_matmul(c):
            codes, scales, first = mx_of[("x", c)]
            words = slice(first, first + width_of(c))
            h_ps_of[c] = []
            for m in range(PACK):
                h_ps = front_psum.tile([P, width_of(c)], F32, tag="front")
                nc.tensor.matmul_mx(
                    out=h_ps[:],
                    lhsT=w1_codes[:, m * P : (m + 1) * P].bitcast(FP8X4),
                    lhsT_scale=w1_scales[:, m * P : (m + 1) * P],
                    rhs=codes[:, words].bitcast(FP8X4),
                    rhs_scale=scales[:, words],
                    start=True,
                    stop=True,
                )
                h_ps_of[c].append(h_ps)

        def relu(c):
            h_planes = work.tile([P, PACK, width_of(c)], BF16)
            for m in range(PACK):
                nc.scalar.activation(
                    out=h_planes[:, m, :], in_=h_ps_of[c][m][:], func=ACT.Relu, bias=b1_cols[:, m : m + 1], scale=1.0
                )
            h_planes_of[c] = h_planes

        def regroup_h(c, copy):
            k, first, last = h_slot(c)
            copy(
                out=grouped_of[k][:, first:last, :].rearrange("p (c i) t -> p c t i", i=4),
                in_=h_planes_of[c][:].rearrange("p t (c i) -> p c t i", i=4),
            )

        def add_bias_to_x(c, j):
            xb = per_tile.tile([P, D], F32)
            nc.gpsimd.tensor_tensor(out=xb[:], in0=x_of(c)[:, j, :], in1=b2_all[:], op=ALU.add)
            xb_of[(c, j)] = xb

        def start_residual(c):
            r = work.tile([P, CHUNK_TILES[c], D], F32)
            r_sum = small.tile([P, CHUNK_TILES[c]], F32)
            r_of[c] = r
            r_sum_of[c] = r_sum

        def second_matmul(c, j):
            codes, scales, first = mx_of[("h", c)]
            words = slice(first + j * P, first + (j + 1) * P)
            y_ps = y_psum.tile([P, D], F32)
            nc.tensor.matmul_mx(
                out=y_ps[:],
                lhsT=codes[:, words].bitcast(FP8X4),
                lhsT_scale=scales[:, words],
                rhs=w2_codes[:].bitcast(FP8X4),
                rhs_scale=w2_scales[:],
                start=True,
                stop=True,
            )
            nc.vector.scalar_tensor_tensor(
                out=r_of[c][:, j, :],
                in0=y_ps[:],
                scalar=0.0,
                in1=xb_of[(c, j)][:],
                op0=ALU.add,
                op1=ALU.add,
                accum_out=r_sum_of[c][:, j : j + 1],
            )

        def negate_mean(c, engine):
            neg_mean = small.tile([P, CHUNK_TILES[c]], F32)
            engine.tensor_scalar_mul(out=neg_mean[:], in0=r_sum_of[c][:], scalar1=-1.0 / D)
            neg_mean_of[c] = neg_mean

        def gain(c, j):
            nc.vector.scalar_tensor_tensor(
                out=scaled_of[c][:, j, :],
                in0=r_of[c][:, j, :],
                scalar=neg_mean_of[c][:, j : j + 1],
                in1=gain_shift[:, 0, :],
                op0=ALU.add,
                op1=ALU.mult,
            )

        def square(c, j, squares, sq_sum):
            nc.scalar.activation(
                out=squares[:, j, :],
                in_=r_of[c][:, j, :],
                func=ACT.Square,
                bias=neg_mean_of[c][:, j : j + 1],
                scale=1.0,
                accum_out=sq_sum[:, j : j + 1],
            )

        def deviation(rstd, sq_sum, j0, j1):
            nc.scalar.activation(
                out=rstd[:, j0:j1], in_=sq_sum[:, j0:j1], func=ACT.Abs_reciprocal_sqrt, bias=eps_tile[:], scale=1.0 / D
            )

        def shift_and_store(c, j):
            result = per_tile.tile([P, D], F32)
            nc.vector.scalar_tensor_tensor(
                out=result[:],
                in0=scaled_of[c][:, j, :],
                scalar=rstd_of[c][:, j : j + 1],
                in1=gain_shift[:, 1, :],
                op0=ALU.mult,
                op1=ALU.add,
            )
            nc.sync.dma_start(out=rows_of(out_flat, c)[:, j, :], in_=result[:])

        def scale_shift_and_store(c, j):
            normed = per_tile.tile([P, D], F32, tag="normed", bufs=2)
            nc.scalar.activation(
                out=normed[:], in_=scaled_of[c][:, j, :], func=ACT.Copy, scale=rstd_of[c][:, j : j + 1]
            )
            shifted = per_tile.tile([P, D], F32, tag="shifted", bufs=3)
            nc.gpsimd.tensor_tensor(out=shifted[:], in0=normed[:], in1=be2_all[:], op=ALU.add)
            nc.sync.dma_start(out=rows_of(out_flat, c)[:, j, :], in_=shifted[:])

        def offloaded(c):
            return 1 + max(0, c - (LAST - 3)) if CHUNK_TILES[c] == 4 else 0

        def quantise_step(k):
            h_width, x_width = width_of(k + 1), width_of(k + 3)
            if h_width == x_width:
                codes, scales = quantise(k, 0, h_width + x_width)
                mx_of[("h", k + 1)] = (codes, scales, 0)
                mx_of[("x", k + 3)] = (codes, scales, h_width)
            else:
                if h_width > 0:
                    mx_of[("h", k + 1)] = quantise(k, 0, h_width) + (0,)
                if x_width > 0:
                    mx_of[("x", k + 3)] = quantise(k, h_width, h_width + x_width) + (0,)

        def step(k):
            has_residual = k <= LAST
            tiles = CHUNK_TILES[k] if has_residual else 0
            next_tiles = CHUNK_TILES[k + 1] if k < LAST else 0
            if k >= LAST - 1:
                for j in range(CHUNK_TILES[k - 1] - offloaded(k - 1), CHUNK_TILES[k - 1]):
                    scale_shift_and_store(k - 1, j)
            if has_residual:
                start_residual(k)
            ahead = 2 if k > 0 else 0
            for j in range(max(tiles, min(next_tiles, ahead))):
                if j < tiles:
                    second_matmul(k, j)
                if j < min(next_tiles, ahead):
                    add_bias_to_x(k + 1, j)
            for j in range(ahead, next_tiles):
                add_bias_to_x(k + 1, j)
            if k < LAST:
                regroup_h(k + 1, nc.scalar.copy)
            if k >= 1:
                for j in range(CHUNK_TILES[k - 1] - offloaded(k - 1)):
                    shift_and_store(k - 1, j)
                    if j == 0 and has_residual:
                        negate_mean(k, nc.vector)
            elif has_residual:
                negate_mean(k, nc.vector)
            if k + 2 <= LAST:
                first_matmul(k + 2)
                relu(k + 2)
            if has_residual:
                scaled = work.tile([P, tiles, D], F32)
                scaled_of[k] = scaled
                for j in range(min(tiles, 2)):
                    gain(k, j)
            if k < LAST:
                quantise_step(k)
            if has_residual:
                for j in range(2, tiles):
                    gain(k, j)
                squares = work.tile([P, tiles, D], BF16)
                sq_sum = small.tile([P, tiles], F32)
                rstd = small.tile([P, tiles], F32)
                for j in range(tiles):
                    square(k, j, squares, sq_sum)
                    if k == LAST:
                        deviation(rstd, sq_sum, j, j + 1)
            if 1 <= k < LAST - 1:
                for j in range(CHUNK_TILES[k - 1] - offloaded(k - 1), CHUNK_TILES[k - 1]):
                    scale_shift_and_store(k - 1, j)
            if k + 2 <= LAST:
                start_group(k + 1, width_of(k + 2), width_of(k + 4))
            if k + 4 <= LAST:
                transpose_x(k + 4, nc.vector.tensor_copy if k == 0 else nc.scalar.copy)
            if has_residual:
                if k < LAST:
                    deviation(rstd, sq_sum, 0, tiles)
                rstd_of[k] = rstd

        start_group(-3, 0, width_of(0))
        transpose_x(0, nc.scalar.copy)
        broadcast_b2()
        mx_of[("x", 0)] = quantise(-3, 0, width_of(0)) + (0,)
        start_group(-2, 0, width_of(1))
        transpose_x(1, nc.vector.tensor_copy)
        for j in range(CHUNK_TILES[0]):
            add_bias_to_x(0, j)
        first_matmul(0)
        relu(0)
        mx_of[("x", 1)] = quantise(-2, 0, width_of(1)) + (0,)
        start_group(-1, width_of(0), width_of(2))
        regroup_h(0, nc.scalar.copy)
        broadcast_gain_and_shift()
        nc.scalar.copy(out=be2_all[:], in_=gain_shift[:, 1, :])
        transpose_x(2, nc.vector.tensor_copy)
        mx_of[("h", 0)] = quantise(-1, 0, width_of(0)) + (0,)
        first_matmul(1)
        relu(1)
        group_w2(nc.vector.tensor_copy)
        quantise_w2()
        mx_of[("x", 2)] = quantise(-1, width_of(0), width_of(0) + width_of(2)) + (0,)
        start_group(0, width_of(1), width_of(3))
        transpose_x(3, nc.scalar.copy)
        for k in range(N_CHUNKS + 1):
            step(k)
